import numpy as np
import ml_dtypes


def mxq(x, axis, fmt="e4m3"):
    dtype, down = {"e4m3": (ml_dtypes.float8_e4m3fn, 7), "e5m2": (ml_dtypes.float8_e5m2, 14)}[fmt]
    v = np.moveaxis(np.asarray(x, np.float32).astype(ml_dtypes.bfloat16).astype(np.float64), axis, -1)
    blocks = v.reshape(v.shape[:-1] + (-1, 32))
    amax = np.abs(blocks).max(-1, keepdims=True)
    byte = np.maximum(np.where(amax > 0, np.frexp(amax)[1] - 1 + 127, 0) - down, 1)
    scale = np.exp2(byte - 127.0)
    codes = (blocks / scale).astype(np.float32).astype(dtype).astype(np.float64)
    return np.moveaxis((codes * scale).reshape(v.shape), -1, axis)


WIDE = False


def mx_kscale(k):
    if not WIDE:
        return np.ones(k)
    levels = np.array([10, -10, 5, -5, 0])
    a = np.random.permutation(np.resize(levels, k // 512 * 4)).reshape(k // 512, 4)
    idx = np.arange(k)
    return np.exp2(a[idx // 512, idx % 128 // 32])


BF16 = ml_dtypes.bfloat16


def bf(x):
    return np.asarray(x, np.float32).astype(BF16)


def f64(x):
    return np.asarray(x).astype(np.float64)


B, CIN, HID, FREQ, T, H = 4, 1024, 128, 4, 512, 8
HD = HID * FREQ // H
EPS = 1e-5


def setup_inputs():
    s = mx_kscale(CIN)
    return {"x": bf(np.random.standard_normal((B, CIN, FREQ, T)) * s[None, :, None, None]),
            "qkv_w": bf(np.random.standard_normal((3 * HID, CIN)) / np.sqrt(CIN) / s[None, :]),
            "qkv_b": bf(np.random.standard_normal(3 * HID) * 0.2),
            "qkv_alpha": bf(0.25 + 0.05 * np.random.standard_normal(1)),
            "qkv_gamma": bf(1.0 + 0.1 * np.random.standard_normal((1, 3 * HID, 1, FREQ))),
            "qkv_beta": bf(0.1 * np.random.standard_normal((1, 3 * HID, 1, FREQ)))}


def reference(x, qkv_w, qkv_b, qkv_alpha, qkv_gamma, qkv_beta):
    xt = np.swapaxes(f64(x), -2, -1)
    y = (mxq(f64(qkv_w), 1, "e4m3") @ mxq(xt, 1, "e4m3").reshape(B, CIN, T * FREQ)).reshape(B, 3 * HID, T, FREQ)
    y = y + f64(qkv_b)[None, :, None, None]
    y = np.where(y >= 0, y, f64(qkv_alpha)[0] * y)
    mu = y.mean(axis=(1, 3), keepdims=True)
    var = np.square(y - mu).mean(axis=(1, 3), keepdims=True)
    n = (y - mu) / np.sqrt(var + EPS) * f64(qkv_gamma) + f64(qkv_beta)
    n = np.swapaxes(np.swapaxes(n, 1, 2).reshape(B, T, H, 3 * HD), 1, 2)
    return (np.ascontiguousarray(n[..., :HD]), np.ascontiguousarray(n[..., HD:2 * HD]), np.ascontiguousarray(n[..., 2 * HD:]))

@@ -1,0 +1,265 @@
+from contextlib import ExitStack
+
+import concourse.mybir as mybir
+from concourse.masks import make_identity
+
+F32 = mybir.dt.float32
+BF16 = mybir.dt.bfloat16
+U32 = mybir.dt.uint32
+U8 = mybir.dt.uint8
+FP8X4 = mybir.dt.float8_e4m3fn_x4
+ALU = mybir.AluOpType
+ACT = mybir.ActivationFunctionType
+
+B, CIN, HID, FREQ, T, H = 4, 1024, 128, 4, 512, 8
+OUT_CH = 3 * HID
+HD = HID * FREQ // H
+EPS = 1e-5
+
+P = 128
+PACK = 4
+K_PASS = P * PACK
+PASSES = CIN // K_PASS
+O_TILES = OUT_CH // P
+T_TILES = T // P
+TILES = B * T_TILES
+COLS = OUT_CH * FREQ
+BANK = 512
+
+FLOPS = 2 * OUT_CH * CIN * B * FREQ * T
+
+ROW_BIAS = 0
+ROW_ALPHA = OUT_CH
+ROW_GAMMA = BANK
+ROW_BETA = BANK + COLS
+ROW_COLS = BANK + 2 * COLS
+
+
+def tile_unified2dattentiononframe_pa_t_kernel(
+    tc, x, qkv_w, qkv_b, qkv_alpha, qkv_gamma, qkv_beta, out_0, out_1, out_2
+):
+    nc = tc.nc
+    outs = (out_0, out_1, out_2)
+    with ExitStack() as ctx:
+        const = ctx.enter_context(tc.tile_pool(name="const", bufs=1))
+        raw_pool = ctx.enter_context(tc.tile_pool(name="raw", bufs=2 * PASSES))
+        grouped_pool = ctx.enter_context(tc.tile_pool(name="grouped", bufs=2 * PASSES))
+        code_pool = ctx.enter_context(tc.tile_pool(name="codes", bufs=3))
+        y_pool = ctx.enter_context(tc.tile_pool(name="y", bufs=3))
+        n_pool = ctx.enter_context(tc.tile_pool(name="n", bufs=4))
+        square_pool = ctx.enter_context(tc.tile_pool(name="square", bufs=2))
+        small = ctx.enter_context(tc.tile_pool(name="small", bufs=4))
+        z_pool = ctx.enter_context(tc.psum_pool(name="z", bufs=2 * O_TILES))
+        wt_pool = ctx.enter_context(tc.psum_pool(name="wt", bufs=2))
+
+        raw = {}
+
+        def new_x_tiles(b):
+            for g in range(PASSES):
+                chunk = raw_pool.tile([P, PACK, FREQ, T], BF16, tag="raw", name="chunk")
+                raw[(b, g)] = chunk
+
+        def load_x(b, t_range):
+            for g in range(PASSES):
+                nc.sync.dma_start(
+                    out=raw[(b, g)][:, :, :, t_range],
+                    in_=x[b, g * K_PASS : (g + 1) * K_PASS, :, t_range].rearrange("(p j) f t -> p j f t", j=PACK),
+                )
+
+        w_sb = const.tile([P, O_TILES * CIN], BF16)
+        nc.sync.dma_start(
+            out=w_sb[:].rearrange("p (a c) -> p a c", a=O_TILES),
+            in_=qkv_w.rearrange("(a p) c -> p a c", p=P),
+        )
+        new_x_tiles(0)
+        load_x(0, slice(0, P))
+
+        rows = const.tile([P, ROW_COLS], BF16)
+        nc.vector.memset(rows[:], 0.0)
+        ones = const.tile([P, P], BF16)
+        nc.vector.memset(ones[:], 1.0)
+        eps_t = const.tile([P, 1], F32)
+        nc.vector.memset(eps_t[:], EPS)
+        nc.sync.dma_start(out=rows[0:1, ROW_BIAS : ROW_BIAS + OUT_CH], in_=qkv_b.rearrange("(a o) -> a o", a=1))
+        nc.sync.dma_start(out=rows[0:1, ROW_ALPHA : ROW_ALPHA + 1], in_=qkv_alpha.rearrange("(a o) -> a o", a=1))
+        nc.sync.dma_start(out=rows[0:1, ROW_GAMMA : ROW_GAMMA + COLS], in_=qkv_gamma.rearrange("a o c f -> a (o c f)"))
+        nc.sync.dma_start(out=rows[0:1, ROW_BETA : ROW_BETA + COLS], in_=qkv_beta.rearrange("a o c f -> a (o c f)"))
+        for tt in range(1, T_TILES):
+            load_x(0, slice(tt * P, (tt + 1) * P))
+        new_x_tiles(1)
+        load_x(1, slice(0, T))
+
+        warm = const.tile([P, 1], F32)
+        nc.scalar.activation(out=warm[:], in_=eps_t[:], func=ACT.Sqrt)
+
+        ident = const.tile([P, P], F32)
+        make_identity(nc, ident[:])
+
+        spread = []
+        for k in range(ROW_COLS // BANK):
+            bank = z_pool.tile([P, BANK], F32, tag="z", name="bank")
+            nc.tensor.matmul(out=bank[:], lhsT=ones[:], rhs=rows[:, k * BANK : (k + 1) * BANK], start=True, stop=True)
+            spread.append(bank)
+
+        alpha_t = const.tile([P, 1], F32)
+        nc.vector.tensor_copy(out=alpha_t[:], in_=spread[0][:, ROW_ALPHA : ROW_ALPHA + 1])
+        sign = const.tile([P, 1], F32)
+        nc.vector.tensor_scalar(out=sign[:], in0=alpha_t[:], scalar1=1.0, scalar2=2.0, op0=ALU.is_le, op1=ALU.mult)
+        nc.vector.tensor_scalar(out=sign[:], in0=sign[:], scalar1=-1.0, scalar2=None, op0=ALU.add)
+        bias_s = const.tile([P, COLS], F32)
+        nc.vector.tensor_scalar(
+            out=bias_s[:].rearrange("p (o f) -> p o f", f=FREQ),
+            in0=spread[0][:, ROW_BIAS : ROW_BIAS + OUT_CH].unsqueeze(2).to_broadcast([P, OUT_CH, FREQ]),
+            scalar1=sign[:, 0:1],
+            scalar2=None,
+            op0=ALU.mult,
+        )
+        gamma_s = const.tile([P, COLS], F32)
+        beta_t = const.tile([P, COLS], F32)
+        for k in range(COLS // BANK):
+            cols = slice(k * BANK, (k + 1) * BANK)
+            nc.vector.tensor_scalar(
+                out=gamma_s[:, cols], in0=spread[ROW_GAMMA // BANK + k][:], scalar1=sign[:, 0:1], scalar2=None, op0=ALU.mult
+            )
+            nc.scalar.copy(out=beta_t[:, cols], in_=spread[ROW_BETA // BANK + k][:])
+
+        w_words = w_sb[:].bitcast(F32).rearrange("p (a g q u) -> p a g q u", a=O_TILES, g=PASSES, q=P, u=2)
+        w_grouped = const.tile([P, PASSES * OUT_CH * PACK], BF16, align_bytes=64)
+        w_grouped_words = w_grouped[:].bitcast(F32).rearrange("p (g o u) -> p g o u", g=PASSES, o=OUT_CH, u=2)
+        w_codes = const.tile([P, PASSES, OUT_CH], U32, align_bytes=64)
+        w_scales = const.tile([P, PASSES, OUT_CH], U8, align_bytes=64)
+        for g in range(PASSES):
+            for a in range(O_TILES):
+                wt = wt_pool.tile([P, 2, P], F32, tag="wt")
+                for u in range(2):
+                    nc.tensor.transpose(wt[:, u, :], w_words[:, a, g, :, u], ident[:])
+                nc.vector.tensor_copy(
+                    out=w_grouped_words[:, g, a * P : (a + 1) * P, :], in_=wt[:].rearrange("p u o -> p o u")
+                )
+        for g in range(PASSES):
+            for a in range(O_TILES):
+                first = (g * OUT_CH + a * P) * PACK
+                nc.vector.quantize_mx(
+                    out=w_codes[:, g, a * P : (a + 1) * P].bitcast(FP8X4),
+                    scales=w_scales[:, g, a * P : (a + 1) * P],
+                    in_=w_grouped[:, first : first + P * PACK],
+                )
+
+        grouped = {}
+        x_codes = {}
+        x_scales = {}
+        z_banks = {}
+        y_tiles = {}
+        n_tiles = {}
+        neg_means = {}
+        stds = {}
+
+        def regroup(i):
+            b, tt = divmod(i, T_TILES)
+            for g in range(PASSES):
+                side = grouped_pool.tile([P, FREQ, P, PACK], BF16, tag="grouped", name="side", align_bytes=64)
+                nc.scalar.copy(
+                    out=side[:], in_=raw[(b, g)][:, :, :, tt * P : (tt + 1) * P].rearrange("p j f t -> p f t j")
+                )
+                grouped[(i, g)] = side
+
+        def quantise(i):
+            codes = code_pool.tile([P, PASSES, FREQ * P], U32, tag="codes", align_bytes=64)
+            scales = code_pool.tile([P, PASSES, FREQ * P], U8, tag="scales", align_bytes=64)
+            for g in range(PASSES):
+                nc.vector.quantize_mx(
+                    out=codes[:, g, :].bitcast(FP8X4),
+                    scales=scales[:, g, :],
+                    in_=grouped[(i, g)][:].rearrange("p f t j -> p (f t j)"),
+                )
+            x_codes[i] = codes
+            x_scales[i] = scales
+
+        def multiply(i):
+            for a in range(O_TILES):
+                z = z_pool.tile([P, FREQ, P], F32, tag="z")
+                for f in range(FREQ):
+                    for g in range(PASSES):
+                        nc.tensor.matmul_mx(
+                            out=z[:, f, :],
+                            lhsT=x_codes[i][:, g, f * P : (f + 1) * P].bitcast(FP8X4),
+                            lhsT_scale=x_scales[i][:, g, f * P : (f + 1) * P],
+                            rhs=w_codes[:, g, a * P : (a + 1) * P].bitcast(FP8X4),
+                            rhs_scale=w_scales[:, g, a * P : (a + 1) * P],
+                            start=(g == 0),
+                            stop=(g == PASSES - 1),
+                        )
+                z_banks[(i, a)] = z
+
+        def activate(i):
+            y = y_pool.tile([P, COLS], F32, tag="y")
+            for a in range(O_TILES):
+                cols = slice(a * BANK, (a + 1) * BANK)
+                nc.vector.scalar_tensor_tensor(
+                    out=y[:, cols].rearrange("p (o f) -> p o f", f=FREQ),
+                    in0=z_banks[(i, a)][:].rearrange("p f o -> p o f"),
+                    scalar=sign[:, 0:1],
+                    in1=bias_s[:, cols].rearrange("p (o f) -> p o f", f=FREQ),
+                    op0=ALU.mult,
+                    op1=ALU.add,
+                )
+            total = small.tile([P, 1], F32, tag="total")
+            nc.vector.scalar_tensor_tensor(
+                out=y[:], in0=y[:], scalar=alpha_t[:, 0:1], in1=y[:], op0=ALU.mult, op1=ALU.max, accum_out=total[:]
+            )
+            neg_mean = small.tile([P, 1], F32, tag="neg_mean")
+            nc.vector.tensor_scalar(out=neg_mean[:], in0=total[:], scalar1=-1.0 / COLS, scalar2=None, op0=ALU.mult)
+            y_tiles[i] = y
+            neg_means[i] = neg_mean
+
+        def deviation(i):
+            square = square_pool.tile([P, COLS], BF16, tag="square")
+            total_sq = small.tile([P, 1], F32, tag="total_sq")
+            nc.scalar.activation(
+                out=square[:], in_=y_tiles[i][:], func=ACT.Square, bias=neg_means[i][:, 0:1], scale=1.0, accum_out=total_sq[:]
+            )
+            std = small.tile([P, 1], F32, tag="std")
+            nc.scalar.activation(out=std[:], in_=total_sq[:], func=ACT.Sqrt, bias=eps_t[:, 0:1], scale=1.0 / COLS)
+            stds[i] = std
+
+        def centre_and_gain(i):
+            n = n_pool.tile([P, COLS], F32, tag="n")
+            nc.vector.scalar_tensor_tensor(
+                out=n[:], in0=y_tiles[i][:], scalar=neg_means[i][:, 0:1], in1=gamma_s[:], op0=ALU.add, op1=ALU.mult
+            )
+            n_tiles[i] = n
+
+        def scale_shift_store(i):
+            b, tt = divmod(i, T_TILES)
+            n = n_tiles[i]
+            rstd = small.tile([P, 1], F32, tag="rstd")
+            nc.vector.reciprocal(out=rstd[:], in_=stds[i][:])
+            nc.vector.scalar_tensor_tensor(
+                out=n[:], in0=n[:], scalar=rstd[:, 0:1], in1=beta_t[:], op0=ALU.mult, op1=ALU.add
+            )
+            heads = n[:].rearrange("p (h s d) -> p h s d", h=H, s=len(outs), d=HD)
+            for s, out in enumerate(outs):
+                nc.sync.dma_start(
+                    out=out[b, :, tt * P : (tt + 1) * P, :].rearrange("h t d -> t h d"), in_=heads[:, :, s, :]
+                )
+
+        AHEAD = 2
+        for i in range(AHEAD):
+            regroup(i)
+            quantise(i)
+        for i in range(TILES):
+            nxt = i + AHEAD
+            multiply(i)
+            if nxt < TILES:
+                if nxt % T_TILES == 0 and nxt // T_TILES + 1 < B:
+                    new_x_tiles(nxt // T_TILES + 1)
+                    load_x(nxt // T_TILES + 1, slice(0, T))
+                regroup(nxt)
+            activate(i)
+            deviation(i)
+            centre_and_gain(i)
+            if nxt < TILES:
+                quantise(nxt)
+            if i > 0:
+                scale_shift_store(i - 1)
+        scale_shift_store(TILES - 1)

@@ -244,22 +244,23 @@ def tile_unified2dattentiononframe_pa_t_kernel(
                 )
 
         AHEAD = 2
-        for i in range(AHEAD):
-            regroup(i)
-            quantise(i)
-        for i in range(TILES):
-            nxt = i + AHEAD
-            multiply(i)
-            if nxt < TILES:
-                if nxt % T_TILES == 0 and nxt // T_TILES + 1 < B:
-                    new_x_tiles(nxt // T_TILES + 1)
-                    load_x(nxt // T_TILES + 1, slice(0, T))
-                regroup(nxt)
-            activate(i)
-            deviation(i)
-            centre_and_gain(i)
-            if nxt < TILES:
-                quantise(nxt)
-            if i > 0:
-                scale_shift_store(i - 1)
-        scale_shift_store(TILES - 1)
+        with tc.manual_schedule():
+            for i in range(AHEAD):
+                regroup(i)
+                quantise(i)
+            for i in range(TILES):
+                nxt = i + AHEAD
+                multiply(i)
+                if nxt < TILES:
+                    if nxt % T_TILES == 0 and nxt // T_TILES + 1 < B:
+                        new_x_tiles(nxt // T_TILES + 1)
+                        load_x(nxt // T_TILES + 1, slice(0, T))
+                    regroup(nxt)
+                activate(i)
+                deviation(i)
+                centre_and_gain(i)
+                if nxt < TILES:
+                    quantise(nxt)
+                if i > 0:
+                    scale_shift_store(i - 1)
+            scale_shift_store(TILES - 1)

@@ -50,7 +50,8 @@ def tile_unified2dattentiononframe_pa_t_kernel(
         square_pool = ctx.enter_context(tc.tile_pool(name="square", bufs=2))
         small = ctx.enter_context(tc.tile_pool(name="small", bufs=4))
         z_pool = ctx.enter_context(tc.psum_pool(name="z", bufs=2 * O_TILES))
-        wt_pool = ctx.enter_context(tc.psum_pool(name="wt", bufs=2))
+        setup_pool = ctx.enter_context(tc.psum_pool(name="setup", bufs=2))
+        ctx.enter_context(tc.manual_schedule())
 
         raw = {}
 
@@ -90,39 +91,10 @@ def tile_unified2dattentiononframe_pa_t_kernel(
         load_x(1, slice(0, T))
 
         warm = const.tile([P, 1], F32)
-        nc.scalar.activation(out=warm[:], in_=eps_t[:], func=ACT.Sqrt)
+        nc.scalar.activation(out=warm[:], in_=eps_t[:], func=ACT.Abs_reciprocal_sqrt)
 
         ident = const.tile([P, P], F32)
         make_identity(nc, ident[:])
-
-        spread = []
-        for k in range(ROW_COLS // BANK):
-            bank = z_pool.tile([P, BANK], F32, tag="z", name="bank")
-            nc.tensor.matmul(out=bank[:], lhsT=ones[:], rhs=rows[:, k * BANK : (k + 1) * BANK], start=True, stop=True)
-            spread.append(bank)
-
-        alpha_t = const.tile([P, 1], F32)
-        nc.vector.tensor_copy(out=alpha_t[:], in_=spread[0][:, ROW_ALPHA : ROW_ALPHA + 1])
-        sign = const.tile([P, 1], F32)
-        nc.vector.tensor_scalar(out=sign[:], in0=alpha_t[:], scalar1=1.0, scalar2=2.0, op0=ALU.is_le, op1=ALU.mult)
-        nc.vector.tensor_scalar(out=sign[:], in0=sign[:], scalar1=-1.0, scalar2=None, op0=ALU.add)
-        bias_s = const.tile([P, COLS], F32)
-        nc.vector.tensor_scalar(
-            out=bias_s[:].rearrange("p (o f) -> p o f", f=FREQ),
-            in0=spread[0][:, ROW_BIAS : ROW_BIAS + OUT_CH].unsqueeze(2).to_broadcast([P, OUT_CH, FREQ]),
-            scalar1=sign[:, 0:1],
-            scalar2=None,
-            op0=ALU.mult,
-        )
-        gamma_s = const.tile([P, COLS], F32)
-        beta_t = const.tile([P, COLS], F32)
-        for k in range(COLS // BANK):
-            cols = slice(k * BANK, (k + 1) * BANK)
-            nc.vector.tensor_scalar(
-                out=gamma_s[:, cols], in0=spread[ROW_GAMMA // BANK + k][:], scalar1=sign[:, 0:1], scalar2=None, op0=ALU.mult
-            )
-            nc.scalar.copy(out=beta_t[:, cols], in_=spread[ROW_BETA // BANK + k][:])
-
         w_words = w_sb[:].bitcast(F32).rearrange("p (a g q u) -> p a g q u", a=O_TILES, g=PASSES, q=P, u=2)
         w_grouped = const.tile([P, PASSES * OUT_CH * PACK], BF16, align_bytes=64)
         w_grouped_words = w_grouped[:].bitcast(F32).rearrange("p (g o u) -> p g o u", g=PASSES, o=OUT_CH, u=2)
@@ -130,7 +102,7 @@ def tile_unified2dattentiononframe_pa_t_kernel(
         w_scales = const.tile([P, PASSES, OUT_CH], U8, align_bytes=64)
         for g in range(PASSES):
             for a in range(O_TILES):
-                wt = wt_pool.tile([P, 2, P], F32, tag="wt")
+                wt = setup_pool.tile([P, 2, P], F32, tag="setup", name="wt")
                 for u in range(2):
                     nc.tensor.transpose(wt[:, u, :], w_words[:, a, g, :, u], ident[:])
                 nc.vector.tensor_copy(
@@ -145,35 +117,48 @@ def tile_unified2dattentiononframe_pa_t_kernel(
                     in_=w_grouped[:, first : first + P * PACK],
                 )
 
+        def spread(first_col):
+            bank = setup_pool.tile([P, BANK], F32, tag="setup", name="bank")
+            nc.tensor.matmul(out=bank[:], lhsT=ones[:], rhs=rows[:, first_col : first_col + BANK], start=True, stop=True)
+            return bank
+
+        alpha_t = const.tile([P, 1], F32)
+        sign = const.tile([P, 1], F32)
+        bias_s = const.tile([P, COLS], F32)
+        gamma_s = const.tile([P, COLS], F32)
+        beta_t = const.tile([P, COLS], F32)
+        bias_bank = spread(ROW_BIAS)
+        nc.vector.tensor_copy(out=alpha_t[:], in_=bias_bank[:, ROW_ALPHA : ROW_ALPHA + 1])
+        nc.vector.tensor_scalar(out=sign[:], in0=alpha_t[:], scalar1=1.0, scalar2=2.0, op0=ALU.is_le, op1=ALU.mult)
+        nc.vector.tensor_scalar(out=sign[:], in0=sign[:], scalar1=-1.0, scalar2=None, op0=ALU.add)
+
         grouped = {}
         x_codes = {}
         x_scales = {}
         z_banks = {}
         y_tiles = {}
         n_tiles = {}
+        totals = {}
         neg_means = {}
-        stds = {}
+        rstds = {}
 
-        def regroup(i):
+        def regroup(i, g, copy):
             b, tt = divmod(i, T_TILES)
-            for g in range(PASSES):
-                side = grouped_pool.tile([P, FREQ, P, PACK], BF16, tag="grouped", name="side", align_bytes=64)
-                nc.scalar.copy(
-                    out=side[:], in_=raw[(b, g)][:, :, :, tt * P : (tt + 1) * P].rearrange("p j f t -> p f t j")
-                )
-                grouped[(i, g)] = side
+            side = grouped_pool.tile([P, FREQ, P, PACK], BF16, tag="grouped", name="side", align_bytes=64)
+            copy(out=side[:], in_=raw[(b, g)][:, :, :, tt * P : (tt + 1) * P].rearrange("p j f t -> p f t j"))
+            grouped[(i, g)] = side
 
-        def quantise(i):
-            codes = code_pool.tile([P, PASSES, FREQ * P], U32, tag="codes", align_bytes=64)
-            scales = code_pool.tile([P, PASSES, FREQ * P], U8, tag="scales", align_bytes=64)
-            for g in range(PASSES):
-                nc.vector.quantize_mx(
-                    out=codes[:, g, :].bitcast(FP8X4),
-                    scales=scales[:, g, :],
-                    in_=grouped[(i, g)][:].rearrange("p f t j -> p (f t j)"),
-                )
-            x_codes[i] = codes
-            x_scales[i] = scales
+        def quantise(i, g):
+            if g == 0:
+                codes = code_pool.tile([P, PASSES, FREQ * P], U32, tag="codes", align_bytes=64)
+                scales = code_pool.tile([P, PASSES, FREQ * P], U8, tag="scales", align_bytes=64)
+                x_codes[i] = codes
+                x_scales[i] = scales
+            nc.vector.quantize_mx(
+                out=x_codes[i][:, g, :].bitcast(FP8X4),
+                scales=x_scales[i][:, g, :],
+                in_=grouped[(i, g)][:].rearrange("p f t j -> p (f t j)"),
+            )
 
         def multiply(i):
             for a in range(O_TILES):
@@ -191,8 +176,9 @@ def tile_unified2dattentiononframe_pa_t_kernel(
                         )
                 z_banks[(i, a)] = z
 
-        def activate(i):
+        def add_bias(i):
             y = y_pool.tile([P, COLS], F32, tag="y")
+            y_tiles[i] = y
             for a in range(O_TILES):
                 cols = slice(a * BANK, (a + 1) * BANK)
                 nc.vector.scalar_tensor_tensor(
@@ -203,13 +189,18 @@ def tile_unified2dattentiononframe_pa_t_kernel(
                     op0=ALU.mult,
                     op1=ALU.add,
                 )
+
+        def prelu(i):
+            y = y_tiles[i]
             total = small.tile([P, 1], F32, tag="total")
             nc.vector.scalar_tensor_tensor(
                 out=y[:], in0=y[:], scalar=alpha_t[:, 0:1], in1=y[:], op0=ALU.mult, op1=ALU.max, accum_out=total[:]
             )
+            totals[i] = total
+
+        def mean(i):
             neg_mean = small.tile([P, 1], F32, tag="neg_mean")
-            nc.vector.tensor_scalar(out=neg_mean[:], in0=total[:], scalar1=-1.0 / COLS, scalar2=None, op0=ALU.mult)
-            y_tiles[i] = y
+            nc.vector.tensor_scalar(out=neg_mean[:], in0=totals[i][:], scalar1=-1.0 / COLS, scalar2=None, op0=ALU.mult)
             neg_means[i] = neg_mean
 
         def deviation(i):
@@ -218,9 +209,11 @@ def tile_unified2dattentiononframe_pa_t_kernel(
             nc.scalar.activation(
                 out=square[:], in_=y_tiles[i][:], func=ACT.Square, bias=neg_means[i][:, 0:1], scale=1.0, accum_out=total_sq[:]
             )
-            std = small.tile([P, 1], F32, tag="std")
-            nc.scalar.activation(out=std[:], in_=total_sq[:], func=ACT.Sqrt, bias=eps_t[:, 0:1], scale=1.0 / COLS)
-            stds[i] = std
+            rstd = small.tile([P, 1], F32, tag="rstd")
+            nc.scalar.activation(
+                out=rstd[:], in_=total_sq[:], func=ACT.Abs_reciprocal_sqrt, bias=eps_t[:, 0:1], scale=1.0 / COLS
+            )
+            rstds[i] = rstd
 
         def centre_and_gain(i):
             n = n_pool.tile([P, COLS], F32, tag="n")
@@ -229,38 +222,61 @@ def tile_unified2dattentiononframe_pa_t_kernel(
             )
             n_tiles[i] = n
 
-        def scale_shift_store(i):
+        def scale_shift_store(i, pieces):
             b, tt = divmod(i, T_TILES)
             n = n_tiles[i]
-            rstd = small.tile([P, 1], F32, tag="rstd")
-            nc.vector.reciprocal(out=rstd[:], in_=stds[i][:])
-            nc.vector.scalar_tensor_tensor(
-                out=n[:], in0=n[:], scalar=rstd[:, 0:1], in1=beta_t[:], op0=ALU.mult, op1=ALU.add
-            )
             heads = n[:].rearrange("p (h s d) -> p h s d", h=H, s=len(outs), d=HD)
-            for s, out in enumerate(outs):
-                nc.sync.dma_start(
-                    out=out[b, :, tt * P : (tt + 1) * P, :].rearrange("h t d -> t h d"), in_=heads[:, :, s, :]
+            for piece in range(pieces):
+                cols = slice(piece * COLS // pieces, (piece + 1) * COLS // pieces)
+                hs = slice(piece * H // pieces, (piece + 1) * H // pieces)
+                nc.vector.scalar_tensor_tensor(
+                    out=n[:, cols], in0=n[:, cols], scalar=rstds[i][:, 0:1], in1=beta_t[:, cols], op0=ALU.mult, op1=ALU.add
                 )
+                for s, out in enumerate(outs):
+                    nc.sync.dma_start(
+                        out=out[b, hs, tt * P : (tt + 1) * P, :].rearrange("h t d -> t h d"), in_=heads[:, hs, s, :]
+                    )
 
-        AHEAD = 2
-        with tc.manual_schedule():
-            for i in range(AHEAD):
-                regroup(i)
-                quantise(i)
-            for i in range(TILES):
-                nxt = i + AHEAD
-                multiply(i)
-                if nxt < TILES:
-                    if nxt % T_TILES == 0 and nxt // T_TILES + 1 < B:
-                        new_x_tiles(nxt // T_TILES + 1)
-                        load_x(nxt // T_TILES + 1, slice(0, T))
-                    regroup(nxt)
-                activate(i)
-                deviation(i)
-                centre_and_gain(i)
-                if nxt < TILES:
-                    quantise(nxt)
-                if i > 0:
-                    scale_shift_store(i - 1)
-            scale_shift_store(TILES - 1)
+        LAST_PIECES = 2
+
+        regroup(0, 0, nc.scalar.copy)
+        nc.scalar.activation(
+            out=bias_s[:].rearrange("p (o f) -> p o f", f=FREQ),
+            in_=bias_bank[:, ROW_BIAS : ROW_BIAS + OUT_CH].unsqueeze(2).to_broadcast([P, OUT_CH, FREQ]),
+            func=ACT.Copy,
+            scale=sign[:, 0:1],
+        )
+        regroup(0, 1, nc.vector.tensor_copy)
+        quantise(0, 0)
+        quantise(0, 1)
+        multiply(0)
+        regroup(1, 0, nc.scalar.copy)
+        regroup(1, 1, nc.scalar.copy)
+        for k in range(COLS // BANK):
+            cols = slice(k * BANK, (k + 1) * BANK)
+            nc.scalar.activation(out=gamma_s[:, cols], in_=spread(ROW_GAMMA + k * BANK)[:], func=ACT.Copy, scale=sign[:, 0:1])
+        for k in range(COLS // BANK):
+            cols = slice(k * BANK, (k + 1) * BANK)
+            nc.scalar.copy(out=beta_t[:, cols], in_=spread(ROW_BETA + k * BANK)[:])
+
+        for i in range(TILES):
+            if i + 2 < TILES:
+                b_next, tt_next = divmod(i + 2, T_TILES)
+                if tt_next == 0 and b_next + 1 < B:
+                    new_x_tiles(b_next + 1)
+                    load_x(b_next + 1, slice(0, T))
+                regroup(i + 2, 0, nc.scalar.copy)
+                regroup(i + 2, 1, nc.scalar.copy)
+            add_bias(i)
+            if i + 1 < TILES:
+                quantise(i + 1, 0)
+            prelu(i)
+            if i + 1 < TILES:
+                quantise(i + 1, 1)
+                multiply(i + 1)
+            mean(i)
+            deviation(i)
+            if i > 0:
+                scale_shift_store(i - 1, 1)
+            centre_and_gain(i)
+        scale_shift_store(TILES - 1, LAST_PIECES)

@@ -25,6 +25,8 @@ T_TILES = T // P
 TILES = B * T_TILES
 COLS = OUT_CH * FREQ
 BANK = 512
+HEAD_COLS = COLS // H
+VECTOR_HEADS = 6
 
 FLOPS = 2 * OUT_CH * CIN * B * FREQ * T
 
@@ -145,7 +147,10 @@ def tile_unified2dattentiononframe_pa_t_kernel(
         def regroup(i, g, copy):
             b, tt = divmod(i, T_TILES)
             side = grouped_pool.tile([P, FREQ, P, PACK], BF16, tag="grouped", name="side", align_bytes=64)
-            copy(out=side[:], in_=raw[(b, g)][:, :, :, tt * P : (tt + 1) * P].rearrange("p j f t -> p f t j"))
+            copy(
+                out=side[:].rearrange("p f (c i) j -> p f c j i", i=4),
+                in_=raw[(b, g)][:, :, :, tt * P : (tt + 1) * P].rearrange("p j f (c i) -> p f c j i", i=4),
+            )
             grouped[(i, g)] = side
 
         def quantise(i, g):
@@ -226,9 +231,16 @@ def tile_unified2dattentiononframe_pa_t_kernel(
             b, tt = divmod(i, T_TILES)
             n = n_tiles[i]
             heads = n[:].rearrange("p (h s d) -> p h s d", h=H, s=len(outs), d=HD)
+            rest = slice(VECTOR_HEADS * HEAD_COLS, COLS)
+            nc.gpsimd.tensor_scalar(
+                out=n[:, rest], in0=n[:, rest], scalar1=rstds[i][:, 0:1], scalar2=0.0, op0=ALU.mult, op1=ALU.add
+            )
+            nc.gpsimd.tensor_tensor(out=n[:, rest], in0=n[:, rest], in1=beta_t[:, rest], op=ALU.add)
             for piece in range(pieces):
-                cols = slice(piece * COLS // pieces, (piece + 1) * COLS // pieces)
-                hs = slice(piece * H // pieces, (piece + 1) * H // pieces)
+                first_head = piece * H // pieces
+                end_head = (piece + 1) * H // pieces
+                hs = slice(first_head, end_head)
+                cols = slice(first_head * HEAD_COLS, min(end_head, VECTOR_HEADS) * HEAD_COLS)
                 nc.vector.scalar_tensor_tensor(
                     out=n[:, cols], in0=n[:, cols], scalar=rstds[i][:, 0:1], in1=beta_t[:, cols], op0=ALU.mult, op1=ALU.add
                 )

@@ -26,7 +26,7 @@ TILES = B * T_TILES
 COLS = OUT_CH * FREQ
 BANK = 512
 HEAD_COLS = COLS // H
-VECTOR_HEADS = 6
+VECTOR_HEADS = 2
 
 FLOPS = 2 * OUT_CH * CIN * B * FREQ * T
 
@@ -51,7 +51,8 @@ def tile_unified2dattentiononframe_pa_t_kernel(
         n_pool = ctx.enter_context(tc.tile_pool(name="n", bufs=4))
         square_pool = ctx.enter_context(tc.tile_pool(name="square", bufs=2))
         small = ctx.enter_context(tc.tile_pool(name="small", bufs=4))
-        z_pool = ctx.enter_context(tc.psum_pool(name="z", bufs=2 * O_TILES))
+        z_pool = ctx.enter_context(tc.psum_pool(name="z", bufs=O_TILES))
+        gamma_pool = ctx.enter_context(tc.psum_pool(name="gamma", bufs=1))
         setup_pool = ctx.enter_context(tc.psum_pool(name="setup", bufs=2))
         ctx.enter_context(tc.manual_schedule())
 
@@ -119,20 +120,20 @@ def tile_unified2dattentiononframe_pa_t_kernel(
                     in_=w_grouped[:, first : first + P * PACK],
                 )
 
-        def spread(first_col):
-            bank = setup_pool.tile([P, BANK], F32, tag="setup", name="bank")
-            nc.tensor.matmul(out=bank[:], lhsT=ones[:], rhs=rows[:, first_col : first_col + BANK], start=True, stop=True)
-            return bank
+        def spread(bank, factor, first_col):
+            nc.tensor.matmul(out=bank[:], lhsT=factor[:], rhs=rows[:, first_col : first_col + BANK], start=True, stop=True)
 
         alpha_t = const.tile([P, 1], F32)
         sign = const.tile([P, 1], F32)
         bias_s = const.tile([P, COLS], F32)
-        gamma_s = const.tile([P, COLS], F32)
         beta_t = const.tile([P, COLS], F32)
-        bias_bank = spread(ROW_BIAS)
+        bias_bank = setup_pool.tile([P, BANK], F32, tag="setup")
+        spread(bias_bank, ones, ROW_BIAS)
         nc.vector.tensor_copy(out=alpha_t[:], in_=bias_bank[:, ROW_ALPHA : ROW_ALPHA + 1])
         nc.vector.tensor_scalar(out=sign[:], in0=alpha_t[:], scalar1=1.0, scalar2=2.0, op0=ALU.is_le, op1=ALU.mult)
         nc.vector.tensor_scalar(out=sign[:], in0=sign[:], scalar1=-1.0, scalar2=None, op0=ALU.add)
+        signed_ones = const.tile([P, P], BF16)
+        nc.vector.tensor_scalar(out=signed_ones[:], in0=ones[:], scalar1=sign[:, 0:1], scalar2=None, op0=ALU.mult)
 
         grouped = {}
         x_codes = {}
@@ -147,10 +148,7 @@ def tile_unified2dattentiononframe_pa_t_kernel(
         def regroup(i, g, copy):
             b, tt = divmod(i, T_TILES)
             side = grouped_pool.tile([P, FREQ, P, PACK], BF16, tag="grouped", name="side", align_bytes=64)
-            copy(
-                out=side[:].rearrange("p f (c i) j -> p f c j i", i=4),
-                in_=raw[(b, g)][:, :, :, tt * P : (tt + 1) * P].rearrange("p j f (c i) -> p f c j i", i=4),
-            )
+            copy(out=side[:], in_=raw[(b, g)][:, :, :, tt * P : (tt + 1) * P].rearrange("p j f t -> p f t j"))
             grouped[(i, g)] = side
 
         def quantise(i, g):
@@ -222,32 +220,39 @@ def tile_unified2dattentiononframe_pa_t_kernel(
 
         def centre_and_gain(i):
             n = n_pool.tile([P, COLS], F32, tag="n")
-            nc.vector.scalar_tensor_tensor(
-                out=n[:], in0=y_tiles[i][:], scalar=neg_means[i][:, 0:1], in1=gamma_s[:], op0=ALU.add, op1=ALU.mult
-            )
+            for k in range(COLS // BANK):
+                cols = slice(k * BANK, (k + 1) * BANK)
+                nc.vector.scalar_tensor_tensor(
+                    out=n[:, cols],
+                    in0=y_tiles[i][:, cols],
+                    scalar=neg_means[i][:, 0:1],
+                    in1=gamma_banks[k][:],
+                    op0=ALU.add,
+                    op1=ALU.mult,
+                )
             n_tiles[i] = n
 
-        def scale_shift_store(i, pieces):
-            b, tt = divmod(i, T_TILES)
+        def scale_shift(i, first_head, end_head):
+            cols = slice(first_head * HEAD_COLS, end_head * HEAD_COLS)
             n = n_tiles[i]
-            heads = n[:].rearrange("p (h s d) -> p h s d", h=H, s=len(outs), d=HD)
-            rest = slice(VECTOR_HEADS * HEAD_COLS, COLS)
-            nc.gpsimd.tensor_scalar(
-                out=n[:, rest], in0=n[:, rest], scalar1=rstds[i][:, 0:1], scalar2=0.0, op0=ALU.mult, op1=ALU.add
+            nc.vector.scalar_tensor_tensor(
+                out=n[:, cols], in0=n[:, cols], scalar=rstds[i][:, 0:1], in1=beta_t[:, cols], op0=ALU.mult, op1=ALU.add
             )
-            nc.gpsimd.tensor_tensor(out=n[:, rest], in0=n[:, rest], in1=beta_t[:, rest], op=ALU.add)
-            for piece in range(pieces):
-                first_head = piece * H // pieces
-                end_head = (piece + 1) * H // pieces
-                hs = slice(first_head, end_head)
-                cols = slice(first_head * HEAD_COLS, min(end_head, VECTOR_HEADS) * HEAD_COLS)
-                nc.vector.scalar_tensor_tensor(
-                    out=n[:, cols], in0=n[:, cols], scalar=rstds[i][:, 0:1], in1=beta_t[:, cols], op0=ALU.mult, op1=ALU.add
+
+        def scale_then_shift_on_gpsimd(i, first_head, end_head):
+            cols = slice(first_head * HEAD_COLS, end_head * HEAD_COLS)
+            n = n_tiles[i]
+            nc.vector.tensor_scalar(out=n[:, cols], in0=n[:, cols], scalar1=rstds[i][:, 0:1], scalar2=None, op0=ALU.mult)
+            nc.gpsimd.tensor_tensor(out=n[:, cols], in0=n[:, cols], in1=beta_t[:, cols], op=ALU.add)
+
+        def store(i, first_head, end_head):
+            b, tt = divmod(i, T_TILES)
+            heads = n_tiles[i][:].rearrange("p (h s d) -> p h s d", h=H, s=len(outs), d=HD)
+            for s, out in enumerate(outs):
+                nc.sync.dma_start(
+                    out=out[b, first_head:end_head, tt * P : (tt + 1) * P, :].rearrange("h t d -> t h d"),
+                    in_=heads[:, first_head:end_head, s, :],
                 )
-                for s, out in enumerate(outs):
-                    nc.sync.dma_start(
-                        out=out[b, hs, tt * P : (tt + 1) * P, :].rearrange("h t d -> t h d"), in_=heads[:, hs, s, :]
-                    )
 
         LAST_PIECES = 2
 
@@ -264,12 +269,15 @@ def tile_unified2dattentiononframe_pa_t_kernel(
         multiply(0)
         regroup(1, 0, nc.scalar.copy)
         regroup(1, 1, nc.scalar.copy)
+        gamma_banks = []
         for k in range(COLS // BANK):
-            cols = slice(k * BANK, (k + 1) * BANK)
-            nc.scalar.activation(out=gamma_s[:, cols], in_=spread(ROW_GAMMA + k * BANK)[:], func=ACT.Copy, scale=sign[:, 0:1])
+            gamma_bank = gamma_pool.tile([P, BANK], F32, tag="gamma%d" % k, name="gamma_bank")
+            spread(gamma_bank, signed_ones, ROW_GAMMA + k * BANK)
+            gamma_banks.append(gamma_bank)
         for k in range(COLS // BANK):
-            cols = slice(k * BANK, (k + 1) * BANK)
-            nc.scalar.copy(out=beta_t[:, cols], in_=spread(ROW_BETA + k * BANK)[:])
+            beta_bank = setup_pool.tile([P, BANK], F32, tag="setup")
+            spread(beta_bank, ones, ROW_BETA + k * BANK)
+            nc.scalar.copy(out=beta_t[:, k * BANK : (k + 1) * BANK], in_=beta_bank[:])
 
         for i in range(TILES):
             if i + 2 < TILES:
@@ -289,6 +297,10 @@ def tile_unified2dattentiononframe_pa_t_kernel(
             mean(i)
             deviation(i)
             if i > 0:
-                scale_shift_store(i - 1, 1)
+                scale_shift(i - 1, 0, VECTOR_HEADS)
+                scale_then_shift_on_gpsimd(i - 1, VECTOR_HEADS, H)
+                store(i - 1, 0, H)
             centre_and_gain(i)
-        scale_shift_store(TILES - 1, LAST_PIECES)
+        for piece in range(LAST_PIECES):
+            scale_shift(TILES - 1, piece * H // LAST_PIECES, (piece + 1) * H // LAST_PIECES)
+            store(TILES - 1, piece * H // LAST_PIECES, (piece + 1) * H // LAST_PIECES)

@@ -20,13 +20,16 @@ P = 128
 PACK = 4
 K_PASS = P * PACK
 PASSES = CIN // K_PASS
-O_TILES = OUT_CH // P
-T_TILES = T // P
-TILES = B * T_TILES
+O_BLOCKS = OUT_CH // P
+T_BLOCKS = T // P
+UNITS = B * T_BLOCKS
 COLS = OUT_CH * FREQ
 BANK = 512
+BANKS = COLS // BANK
 HEAD_COLS = COLS // H
+
 VECTOR_HEADS = 2
+LAST_PIECES = 4
 
 FLOPS = 2 * OUT_CH * CIN * B * FREQ * T
 
@@ -49,9 +52,9 @@ def tile_unified2dattentiononframe_pa_t_kernel(
         code_pool = ctx.enter_context(tc.tile_pool(name="codes", bufs=3))
         y_pool = ctx.enter_context(tc.tile_pool(name="y", bufs=3))
         n_pool = ctx.enter_context(tc.tile_pool(name="n", bufs=4))
-        square_pool = ctx.enter_context(tc.tile_pool(name="square", bufs=2))
         small = ctx.enter_context(tc.tile_pool(name="small", bufs=4))
-        z_pool = ctx.enter_context(tc.psum_pool(name="z", bufs=O_TILES))
+        square_pool = ctx.enter_context(tc.tile_pool(name="square", bufs=2))
+        z_pool = ctx.enter_context(tc.psum_pool(name="z", bufs=BANKS))
         gamma_pool = ctx.enter_context(tc.psum_pool(name="gamma", bufs=1))
         setup_pool = ctx.enter_context(tc.psum_pool(name="setup", bufs=2))
         ctx.enter_context(tc.manual_schedule())
@@ -70,9 +73,9 @@ def tile_unified2dattentiononframe_pa_t_kernel(
                     in_=x[b, g * K_PASS : (g + 1) * K_PASS, :, t_range].rearrange("(p j) f t -> p j f t", j=PACK),
                 )
 
-        w_sb = const.tile([P, O_TILES * CIN], BF16)
+        w_sb = const.tile([P, O_BLOCKS * CIN], BF16)
         nc.sync.dma_start(
-            out=w_sb[:].rearrange("p (a c) -> p a c", a=O_TILES),
+            out=w_sb[:].rearrange("p (a c) -> p a c", a=O_BLOCKS),
             in_=qkv_w.rearrange("(a p) c -> p a c", p=P),
         )
         new_x_tiles(0)
@@ -84,11 +87,12 @@ def tile_unified2dattentiononframe_pa_t_kernel(
         nc.vector.memset(ones[:], 1.0)
         eps_t = const.tile([P, 1], F32)
         nc.vector.memset(eps_t[:], EPS)
-        nc.sync.dma_start(out=rows[0:1, ROW_BIAS : ROW_BIAS + OUT_CH], in_=qkv_b.rearrange("(a o) -> a o", a=1))
-        nc.sync.dma_start(out=rows[0:1, ROW_ALPHA : ROW_ALPHA + 1], in_=qkv_alpha.rearrange("(a o) -> a o", a=1))
-        nc.sync.dma_start(out=rows[0:1, ROW_GAMMA : ROW_GAMMA + COLS], in_=qkv_gamma.rearrange("a o c f -> a (o c f)"))
-        nc.sync.dma_start(out=rows[0:1, ROW_BETA : ROW_BETA + COLS], in_=qkv_beta.rearrange("a o c f -> a (o c f)"))
-        for tt in range(1, T_TILES):
+        nc.sync.dma_start(out=rows[0:1, ROW_BIAS : ROW_BIAS + OUT_CH], in_=qkv_b.rearrange("(r o) -> r o", r=1))
+        nc.sync.dma_start(out=rows[0:1, ROW_ALPHA : ROW_ALPHA + 1], in_=qkv_alpha.rearrange("(r o) -> r o", r=1))
+        nc.sync.dma_start(out=rows[0:1, ROW_GAMMA : ROW_GAMMA + COLS], in_=qkv_gamma.rearrange("r o c f -> r (o c f)"))
+        nc.sync.dma_start(out=rows[0:1, ROW_BETA : ROW_BETA + COLS], in_=qkv_beta.rearrange("r o c f -> r (o c f)"))
+
+        for tt in range(1, T_BLOCKS):
             load_x(0, slice(tt * P, (tt + 1) * P))
         new_x_tiles(1)
         load_x(1, slice(0, T))
@@ -98,13 +102,13 @@ def tile_unified2dattentiononframe_pa_t_kernel(
 
         ident = const.tile([P, P], F32)
         make_identity(nc, ident[:])
-        w_words = w_sb[:].bitcast(F32).rearrange("p (a g q u) -> p a g q u", a=O_TILES, g=PASSES, q=P, u=2)
+        w_words = w_sb[:].bitcast(F32).rearrange("p (a g q u) -> p a g q u", a=O_BLOCKS, g=PASSES, q=P, u=2)
         w_grouped = const.tile([P, PASSES * OUT_CH * PACK], BF16, align_bytes=64)
         w_grouped_words = w_grouped[:].bitcast(F32).rearrange("p (g o u) -> p g o u", g=PASSES, o=OUT_CH, u=2)
         w_codes = const.tile([P, PASSES, OUT_CH], U32, align_bytes=64)
         w_scales = const.tile([P, PASSES, OUT_CH], U8, align_bytes=64)
         for g in range(PASSES):
-            for a in range(O_TILES):
+            for a in range(O_BLOCKS):
                 wt = setup_pool.tile([P, 2, P], F32, tag="setup", name="wt")
                 for u in range(2):
                     nc.tensor.transpose(wt[:, u, :], w_words[:, a, g, :, u], ident[:])
@@ -112,7 +116,7 @@ def tile_unified2dattentiononframe_pa_t_kernel(
                     out=w_grouped_words[:, g, a * P : (a + 1) * P, :], in_=wt[:].rearrange("p u o -> p o u")
                 )
         for g in range(PASSES):
-            for a in range(O_TILES):
+            for a in range(O_BLOCKS):
                 first = (g * OUT_CH + a * P) * PACK
                 nc.vector.quantize_mx(
                     out=w_codes[:, g, a * P : (a + 1) * P].bitcast(FP8X4),
@@ -144,9 +148,10 @@ def tile_unified2dattentiononframe_pa_t_kernel(
         totals = {}
         neg_means = {}
         rstds = {}
+        gamma_banks = []
 
         def regroup(i, g, copy):
-            b, tt = divmod(i, T_TILES)
+            b, tt = divmod(i, T_BLOCKS)
             side = grouped_pool.tile([P, FREQ, P, PACK], BF16, tag="grouped", name="side", align_bytes=64)
             copy(out=side[:], in_=raw[(b, g)][:, :, :, tt * P : (tt + 1) * P].rearrange("p j f t -> p f t j"))
             grouped[(i, g)] = side
@@ -164,7 +169,7 @@ def tile_unified2dattentiononframe_pa_t_kernel(
             )
 
         def multiply(i):
-            for a in range(O_TILES):
+            for a in range(O_BLOCKS):
                 z = z_pool.tile([P, FREQ, P], F32, tag="z")
                 for f in range(FREQ):
                     for g in range(PASSES):
@@ -182,7 +187,7 @@ def tile_unified2dattentiononframe_pa_t_kernel(
         def add_bias(i):
             y = y_pool.tile([P, COLS], F32, tag="y")
             y_tiles[i] = y
-            for a in range(O_TILES):
+            for a in range(O_BLOCKS):
                 cols = slice(a * BANK, (a + 1) * BANK)
                 nc.vector.scalar_tensor_tensor(
                     out=y[:, cols].rearrange("p (o f) -> p o f", f=FREQ),
@@ -220,7 +225,7 @@ def tile_unified2dattentiononframe_pa_t_kernel(
 
         def centre_and_gain(i):
             n = n_pool.tile([P, COLS], F32, tag="n")
-            for k in range(COLS // BANK):
+            for k in range(BANKS):
                 cols = slice(k * BANK, (k + 1) * BANK)
                 nc.vector.scalar_tensor_tensor(
                     out=n[:, cols],
@@ -232,7 +237,7 @@ def tile_unified2dattentiononframe_pa_t_kernel(
                 )
             n_tiles[i] = n
 
-        def scale_shift(i, first_head, end_head):
+        def scale_and_shift(i, first_head, end_head):
             cols = slice(first_head * HEAD_COLS, end_head * HEAD_COLS)
             n = n_tiles[i]
             nc.vector.scalar_tensor_tensor(
@@ -246,15 +251,13 @@ def tile_unified2dattentiononframe_pa_t_kernel(
             nc.gpsimd.tensor_tensor(out=n[:, cols], in0=n[:, cols], in1=beta_t[:, cols], op=ALU.add)
 
         def store(i, first_head, end_head):
-            b, tt = divmod(i, T_TILES)
+            b, tt = divmod(i, T_BLOCKS)
             heads = n_tiles[i][:].rearrange("p (h s d) -> p h s d", h=H, s=len(outs), d=HD)
             for s, out in enumerate(outs):
                 nc.sync.dma_start(
                     out=out[b, first_head:end_head, tt * P : (tt + 1) * P, :].rearrange("h t d -> t h d"),
                     in_=heads[:, first_head:end_head, s, :],
                 )
-
-        LAST_PIECES = 2
 
         regroup(0, 0, nc.scalar.copy)
         nc.scalar.activation(
@@ -269,38 +272,42 @@ def tile_unified2dattentiononframe_pa_t_kernel(
         multiply(0)
         regroup(1, 0, nc.scalar.copy)
         regroup(1, 1, nc.scalar.copy)
-        gamma_banks = []
-        for k in range(COLS // BANK):
+        for k in range(BANKS):
             gamma_bank = gamma_pool.tile([P, BANK], F32, tag="gamma%d" % k, name="gamma_bank")
             spread(gamma_bank, signed_ones, ROW_GAMMA + k * BANK)
             gamma_banks.append(gamma_bank)
-        for k in range(COLS // BANK):
+        for k in range(BANKS):
             beta_bank = setup_pool.tile([P, BANK], F32, tag="setup")
             spread(beta_bank, ones, ROW_BETA + k * BANK)
             nc.scalar.copy(out=beta_t[:, k * BANK : (k + 1) * BANK], in_=beta_bank[:])
 
-        for i in range(TILES):
-            if i + 2 < TILES:
-                b_next, tt_next = divmod(i + 2, T_TILES)
+        for i in range(UNITS):
+            if i + 2 < UNITS:
+                b_next, tt_next = divmod(i + 2, T_BLOCKS)
                 if tt_next == 0 and b_next + 1 < B:
                     new_x_tiles(b_next + 1)
                     load_x(b_next + 1, slice(0, T))
                 regroup(i + 2, 0, nc.scalar.copy)
                 regroup(i + 2, 1, nc.scalar.copy)
             add_bias(i)
-            if i + 1 < TILES:
+            if i + 1 < UNITS:
                 quantise(i + 1, 0)
             prelu(i)
-            if i + 1 < TILES:
+            if i + 1 < UNITS:
                 quantise(i + 1, 1)
                 multiply(i + 1)
             mean(i)
             deviation(i)
-            if i > 0:
-                scale_shift(i - 1, 0, VECTOR_HEADS)
+            if 0 < i < UNITS - 1:
+                scale_and_shift(i - 1, 0, VECTOR_HEADS)
                 scale_then_shift_on_gpsimd(i - 1, VECTOR_HEADS, H)
+                store(i - 1, 0, H)
+            if i == UNITS - 1:
+                scale_and_shift(i - 1, 0, H)
                 store(i - 1, 0, H)
             centre_and_gain(i)
         for piece in range(LAST_PIECES):
-            scale_shift(TILES - 1, piece * H // LAST_PIECES, (piece + 1) * H // LAST_PIECES)
-            store(TILES - 1, piece * H // LAST_PIECES, (piece + 1) * H // LAST_PIECES)
+            first_head = piece * H // LAST_PIECES
+            end_head = (piece + 1) * H // LAST_PIECES
+            scale_and_shift(UNITS - 1, first_head, end_head)
+            store(UNITS - 1, first_head, end_head)

@@ -20,9 +20,10 @@ P = 128
 PACK = 4
 K_PASS = P * PACK
 PASSES = CIN // K_PASS
-O_BLOCKS = OUT_CH // P
-T_BLOCKS = T // P
-UNITS = B * T_BLOCKS
+PAIRS = PACK // 2
+O_STRIPES = OUT_CH // P
+T_STRIPES = T // P
+UNITS = B * T_STRIPES
 COLS = OUT_CH * FREQ
 BANK = 512
 BANKS = COLS // BANK
@@ -73,9 +74,9 @@ def tile_unified2dattentiononframe_pa_t_kernel(
                     in_=x[b, g * K_PASS : (g + 1) * K_PASS, :, t_range].rearrange("(p j) f t -> p j f t", j=PACK),
                 )
 
-        w_sb = const.tile([P, O_BLOCKS * CIN], BF16)
+        w_sb = const.tile([P, O_STRIPES * CIN], BF16)
         nc.sync.dma_start(
-            out=w_sb[:].rearrange("p (a c) -> p a c", a=O_BLOCKS),
+            out=w_sb[:].rearrange("p (a c) -> p a c", a=O_STRIPES),
             in_=qkv_w.rearrange("(a p) c -> p a c", p=P),
         )
         new_x_tiles(0)
@@ -87,12 +88,12 @@ def tile_unified2dattentiononframe_pa_t_kernel(
         nc.vector.memset(ones[:], 1.0)
         eps_t = const.tile([P, 1], F32)
         nc.vector.memset(eps_t[:], EPS)
-        nc.sync.dma_start(out=rows[0:1, ROW_BIAS : ROW_BIAS + OUT_CH], in_=qkv_b.rearrange("(r o) -> r o", r=1))
-        nc.sync.dma_start(out=rows[0:1, ROW_ALPHA : ROW_ALPHA + 1], in_=qkv_alpha.rearrange("(r o) -> r o", r=1))
-        nc.sync.dma_start(out=rows[0:1, ROW_GAMMA : ROW_GAMMA + COLS], in_=qkv_gamma.rearrange("r o c f -> r (o c f)"))
-        nc.sync.dma_start(out=rows[0:1, ROW_BETA : ROW_BETA + COLS], in_=qkv_beta.rearrange("r o c f -> r (o c f)"))
+        nc.scalar.dma_start(out=rows[0:1, ROW_BIAS : ROW_BIAS + OUT_CH], in_=qkv_b.rearrange("(r o) -> r o", r=1))
+        nc.scalar.dma_start(out=rows[0:1, ROW_ALPHA : ROW_ALPHA + 1], in_=qkv_alpha.rearrange("(r o) -> r o", r=1))
+        nc.scalar.dma_start(out=rows[0:1, ROW_GAMMA : ROW_GAMMA + COLS], in_=qkv_gamma.rearrange("r o c f -> r (o c f)"))
+        nc.scalar.dma_start(out=rows[0:1, ROW_BETA : ROW_BETA + COLS], in_=qkv_beta.rearrange("r o c f -> r (o c f)"))
 
-        for tt in range(1, T_BLOCKS):
+        for tt in range(1, T_STRIPES):
             load_x(0, slice(tt * P, (tt + 1) * P))
         new_x_tiles(1)
         load_x(1, slice(0, T))
@@ -102,21 +103,21 @@ def tile_unified2dattentiononframe_pa_t_kernel(
 
         ident = const.tile([P, P], F32)
         make_identity(nc, ident[:])
-        w_words = w_sb[:].bitcast(F32).rearrange("p (a g q u) -> p a g q u", a=O_BLOCKS, g=PASSES, q=P, u=2)
+        w_pairs = w_sb[:].bitcast(F32).rearrange("p (a g q u) -> p a g q u", a=O_STRIPES, g=PASSES, q=P, u=PAIRS)
         w_grouped = const.tile([P, PASSES * OUT_CH * PACK], BF16, align_bytes=64)
-        w_grouped_words = w_grouped[:].bitcast(F32).rearrange("p (g o u) -> p g o u", g=PASSES, o=OUT_CH, u=2)
+        w_grouped_pairs = w_grouped[:].bitcast(F32).rearrange("p (g o u) -> p g o u", g=PASSES, o=OUT_CH, u=PAIRS)
         w_codes = const.tile([P, PASSES, OUT_CH], U32, align_bytes=64)
         w_scales = const.tile([P, PASSES, OUT_CH], U8, align_bytes=64)
         for g in range(PASSES):
-            for a in range(O_BLOCKS):
-                wt = setup_pool.tile([P, 2, P], F32, tag="setup", name="wt")
-                for u in range(2):
-                    nc.tensor.transpose(wt[:, u, :], w_words[:, a, g, :, u], ident[:])
+            for a in range(O_STRIPES):
+                wt = setup_pool.tile([P, PAIRS, P], F32, tag="setup", name="wt")
+                for u in range(PAIRS):
+                    nc.tensor.transpose(wt[:, u, :], w_pairs[:, a, g, :, u], ident[:])
                 nc.vector.tensor_copy(
-                    out=w_grouped_words[:, g, a * P : (a + 1) * P, :], in_=wt[:].rearrange("p u o -> p o u")
+                    out=w_grouped_pairs[:, g, a * P : (a + 1) * P, :], in_=wt[:].rearrange("p u o -> p o u")
                 )
         for g in range(PASSES):
-            for a in range(O_BLOCKS):
+            for a in range(O_STRIPES):
                 first = (g * OUT_CH + a * P) * PACK
                 nc.vector.quantize_mx(
                     out=w_codes[:, g, a * P : (a + 1) * P].bitcast(FP8X4),
@@ -151,7 +152,7 @@ def tile_unified2dattentiononframe_pa_t_kernel(
         gamma_banks = []
 
         def regroup(i, g, copy):
-            b, tt = divmod(i, T_BLOCKS)
+            b, tt = divmod(i, T_STRIPES)
             side = grouped_pool.tile([P, FREQ, P, PACK], BF16, tag="grouped", name="side", align_bytes=64)
             copy(out=side[:], in_=raw[(b, g)][:, :, :, tt * P : (tt + 1) * P].rearrange("p j f t -> p f t j"))
             grouped[(i, g)] = side
@@ -169,7 +170,7 @@ def tile_unified2dattentiononframe_pa_t_kernel(
             )
 
         def multiply(i):
-            for a in range(O_BLOCKS):
+            for a in range(O_STRIPES):
                 z = z_pool.tile([P, FREQ, P], F32, tag="z")
                 for f in range(FREQ):
                     for g in range(PASSES):
@@ -187,7 +188,7 @@ def tile_unified2dattentiononframe_pa_t_kernel(
         def add_bias(i):
             y = y_pool.tile([P, COLS], F32, tag="y")
             y_tiles[i] = y
-            for a in range(O_BLOCKS):
+            for a in range(O_STRIPES):
                 cols = slice(a * BANK, (a + 1) * BANK)
                 nc.vector.scalar_tensor_tensor(
                     out=y[:, cols].rearrange("p (o f) -> p o f", f=FREQ),
@@ -251,7 +252,7 @@ def tile_unified2dattentiononframe_pa_t_kernel(
             nc.gpsimd.tensor_tensor(out=n[:, cols], in0=n[:, cols], in1=beta_t[:, cols], op=ALU.add)
 
         def store(i, first_head, end_head):
-            b, tt = divmod(i, T_BLOCKS)
+            b, tt = divmod(i, T_STRIPES)
             heads = n_tiles[i][:].rearrange("p (h s d) -> p h s d", h=H, s=len(outs), d=HD)
             for s, out in enumerate(outs):
                 nc.sync.dma_start(
@@ -283,7 +284,7 @@ def tile_unified2dattentiononframe_pa_t_kernel(
 
         for i in range(UNITS):
             if i + 2 < UNITS:
-                b_next, tt_next = divmod(i + 2, T_BLOCKS)
+                b_next, tt_next = divmod(i + 2, T_STRIPES)
                 if tt_next == 0 and b_next + 1 < B:
                     new_x_tiles(b_next + 1)
                     load_x(b_next + 1, slice(0, T))

@@ -31,6 +31,7 @@ HEAD_COLS = COLS // H
 
 VECTOR_HEADS = 2
 LAST_PIECES = 4
+VECTOR_STEPS = 96
 
 FLOPS = 2 * OUT_CH * CIN * B * FREQ * T
 
@@ -51,12 +52,13 @@ def tile_unified2dattentiononframe_pa_t_kernel(
         raw_pool = ctx.enter_context(tc.tile_pool(name="raw", bufs=2 * PASSES))
         grouped_pool = ctx.enter_context(tc.tile_pool(name="grouped", bufs=2 * PASSES))
         code_pool = ctx.enter_context(tc.tile_pool(name="codes", bufs=3))
-        y_pool = ctx.enter_context(tc.tile_pool(name="y", bufs=3))
+        slope_pool = ctx.enter_context(tc.tile_pool(name="slope", bufs=2))
+        p_pool = ctx.enter_context(tc.tile_pool(name="p", bufs=2))
         n_pool = ctx.enter_context(tc.tile_pool(name="n", bufs=4))
         small = ctx.enter_context(tc.tile_pool(name="small", bufs=4))
         square_pool = ctx.enter_context(tc.tile_pool(name="square", bufs=2))
         z_pool = ctx.enter_context(tc.psum_pool(name="z", bufs=BANKS))
-        gamma_pool = ctx.enter_context(tc.psum_pool(name="gamma", bufs=1))
+        pt_pool = ctx.enter_context(tc.psum_pool(name="pt", bufs=BANKS))
         setup_pool = ctx.enter_context(tc.psum_pool(name="setup", bufs=2))
         ctx.enter_context(tc.manual_schedule())
 
@@ -74,6 +76,12 @@ def tile_unified2dattentiononframe_pa_t_kernel(
                     in_=x[b, g * K_PASS : (g + 1) * K_PASS, :, t_range].rearrange("(p j) f t -> p j f t", j=PACK),
                 )
 
+        rows = const.tile([P, ROW_COLS], BF16)
+        nc.vector.memset(rows[:], 0.0)
+        ones = const.tile([P, P], BF16)
+        nc.vector.memset(ones[:], 1.0)
+        eps_t = const.tile([P, 1], F32)
+        nc.vector.memset(eps_t[:], EPS)
         w_sb = const.tile([P, O_STRIPES * CIN], BF16)
         nc.sync.dma_start(
             out=w_sb[:].rearrange("p (a c) -> p a c", a=O_STRIPES),
@@ -81,18 +89,10 @@ def tile_unified2dattentiononframe_pa_t_kernel(
         )
         new_x_tiles(0)
         load_x(0, slice(0, P))
-
-        rows = const.tile([P, ROW_COLS], BF16)
-        nc.vector.memset(rows[:], 0.0)
-        ones = const.tile([P, P], BF16)
-        nc.vector.memset(ones[:], 1.0)
-        eps_t = const.tile([P, 1], F32)
-        nc.vector.memset(eps_t[:], EPS)
-        nc.scalar.dma_start(out=rows[0:1, ROW_BIAS : ROW_BIAS + OUT_CH], in_=qkv_b.rearrange("(r o) -> r o", r=1))
-        nc.scalar.dma_start(out=rows[0:1, ROW_ALPHA : ROW_ALPHA + 1], in_=qkv_alpha.rearrange("(r o) -> r o", r=1))
-        nc.scalar.dma_start(out=rows[0:1, ROW_GAMMA : ROW_GAMMA + COLS], in_=qkv_gamma.rearrange("r o c f -> r (o c f)"))
-        nc.scalar.dma_start(out=rows[0:1, ROW_BETA : ROW_BETA + COLS], in_=qkv_beta.rearrange("r o c f -> r (o c f)"))
-
+        nc.sync.dma_start(out=rows[0:1, ROW_ALPHA : ROW_ALPHA + 1], in_=qkv_alpha.rearrange("(r o) -> r o", r=1))
+        nc.sync.dma_start(out=rows[0:1, ROW_BIAS : ROW_BIAS + OUT_CH], in_=qkv_b.rearrange("(r o) -> r o", r=1))
+        nc.sync.dma_start(out=rows[0:1, ROW_GAMMA : ROW_GAMMA + COLS], in_=qkv_gamma.rearrange("r o c f -> r (o c f)"))
+        nc.sync.dma_start(out=rows[0:1, ROW_BETA : ROW_BETA + COLS], in_=qkv_beta.rearrange("r o c f -> r (o c f)"))
         for tt in range(1, T_STRIPES):
             load_x(0, slice(tt * P, (tt + 1) * P))
         new_x_tiles(1)
@@ -103,26 +103,20 @@ def tile_unified2dattentiononframe_pa_t_kernel(
 
         ident = const.tile([P, P], F32)
         make_identity(nc, ident[:])
+
         w_pairs = w_sb[:].bitcast(F32).rearrange("p (a g q u) -> p a g q u", a=O_STRIPES, g=PASSES, q=P, u=PAIRS)
         w_grouped = const.tile([P, PASSES * OUT_CH * PACK], BF16, align_bytes=64)
         w_grouped_pairs = w_grouped[:].bitcast(F32).rearrange("p (g o u) -> p g o u", g=PASSES, o=OUT_CH, u=PAIRS)
+        w_signed = const.tile([P, PASSES * OUT_CH * PACK], BF16, align_bytes=64)
         w_codes = const.tile([P, PASSES, OUT_CH], U32, align_bytes=64)
         w_scales = const.tile([P, PASSES, OUT_CH], U8, align_bytes=64)
         for g in range(PASSES):
             for a in range(O_STRIPES):
-                wt = setup_pool.tile([P, PAIRS, P], F32, tag="setup", name="wt")
+                wt = z_pool.tile([P, PAIRS, P], F32, tag="z", name="wt")
                 for u in range(PAIRS):
                     nc.tensor.transpose(wt[:, u, :], w_pairs[:, a, g, :, u], ident[:])
                 nc.vector.tensor_copy(
                     out=w_grouped_pairs[:, g, a * P : (a + 1) * P, :], in_=wt[:].rearrange("p u o -> p o u")
-                )
-        for g in range(PASSES):
-            for a in range(O_STRIPES):
-                first = (g * OUT_CH + a * P) * PACK
-                nc.vector.quantize_mx(
-                    out=w_codes[:, g, a * P : (a + 1) * P].bitcast(FP8X4),
-                    scales=w_scales[:, g, a * P : (a + 1) * P],
-                    in_=w_grouped[:, first : first + P * PACK],
                 )
 
         def spread(bank, factor, first_col):
@@ -130,8 +124,6 @@ def tile_unified2dattentiononframe_pa_t_kernel(
 
         alpha_t = const.tile([P, 1], F32)
         sign = const.tile([P, 1], F32)
-        bias_s = const.tile([P, COLS], F32)
-        beta_t = const.tile([P, COLS], F32)
         bias_bank = setup_pool.tile([P, BANK], F32, tag="setup")
         spread(bias_bank, ones, ROW_BIAS)
         nc.vector.tensor_copy(out=alpha_t[:], in_=bias_bank[:, ROW_ALPHA : ROW_ALPHA + 1])
@@ -139,23 +131,48 @@ def tile_unified2dattentiononframe_pa_t_kernel(
         nc.vector.tensor_scalar(out=sign[:], in0=sign[:], scalar1=-1.0, scalar2=None, op0=ALU.add)
         signed_ones = const.tile([P, P], BF16)
         nc.vector.tensor_scalar(out=signed_ones[:], in0=ones[:], scalar1=sign[:, 0:1], scalar2=None, op0=ALU.mult)
+        bias_cols_bank = setup_pool.tile([P, BANK], F32, tag="setup")
+        for a in range(O_STRIPES):
+            nc.tensor.matmul(
+                out=bias_cols_bank[:, a : a + 1],
+                lhsT=rows[:, ROW_BIAS + a * P : ROW_BIAS + (a + 1) * P],
+                rhs=signed_ones[:, 0:1],
+                start=True,
+                stop=True,
+            )
 
         grouped = {}
         x_codes = {}
         x_scales = {}
         z_banks = {}
-        y_tiles = {}
+        slopes = {}
+        p_tiles = {}
+        pt_banks = {}
+        sums = {}
         n_tiles = {}
-        totals = {}
         neg_means = {}
+        squares = {}
+        totals_sq = {}
         rstds = {}
-        gamma_banks = []
+        gamma_t = const.tile([P, COLS], F32)
+        beta_t = const.tile([P, COLS], F32)
 
-        def regroup(i, g, copy):
+        def regroup(i, g, first_step, end_step, copy):
             b, tt = divmod(i, T_STRIPES)
-            side = grouped_pool.tile([P, FREQ, P, PACK], BF16, tag="grouped", name="side", align_bytes=64)
-            copy(out=side[:], in_=raw[(b, g)][:, :, :, tt * P : (tt + 1) * P].rearrange("p j f t -> p f t j"))
-            grouped[(i, g)] = side
+            if (i, g) not in grouped:
+                side = grouped_pool.tile([P, FREQ, P, PACK], BF16, tag="grouped", name="side", align_bytes=64)
+                grouped[(i, g)] = side
+            copy(
+                out=grouped[(i, g)][:, :, first_step:end_step, :],
+                in_=raw[(b, g)][:, :, :, tt * P + first_step : tt * P + end_step].rearrange("p j f t -> p f t j"),
+            )
+
+        def regroup_on_scalar(i):
+            regroup(i, 0, 0, P, nc.scalar.copy)
+            regroup(i, 1, VECTOR_STEPS, P, nc.scalar.copy)
+
+        def regroup_on_vector(i):
+            regroup(i, 1, 0, VECTOR_STEPS, nc.vector.tensor_copy)
 
         def quantise(i, g):
             if g == 0:
@@ -171,68 +188,107 @@ def tile_unified2dattentiononframe_pa_t_kernel(
 
         def multiply(i):
             for a in range(O_STRIPES):
-                z = z_pool.tile([P, FREQ, P], F32, tag="z")
-                for f in range(FREQ):
-                    for g in range(PASSES):
-                        nc.tensor.matmul_mx(
-                            out=z[:, f, :],
-                            lhsT=x_codes[i][:, g, f * P : (f + 1) * P].bitcast(FP8X4),
-                            lhsT_scale=x_scales[i][:, g, f * P : (f + 1) * P],
-                            rhs=w_codes[:, g, a * P : (a + 1) * P].bitcast(FP8X4),
-                            rhs_scale=w_scales[:, g, a * P : (a + 1) * P],
-                            start=(g == 0),
-                            stop=(g == PASSES - 1),
-                        )
+                z = z_pool.tile([P, BANK], F32, tag="z")
+                for g in range(PASSES):
+                    nc.tensor.matmul_mx(
+                        out=z[:],
+                        lhsT=w_codes[:, g, a * P : (a + 1) * P].bitcast(FP8X4),
+                        lhsT_scale=w_scales[:, g, a * P : (a + 1) * P],
+                        rhs=x_codes[i][:, g, :].bitcast(FP8X4),
+                        rhs_scale=x_scales[i][:, g, :],
+                        start=(g == 0),
+                        stop=(g == PASSES - 1),
+                    )
                 z_banks[(i, a)] = z
 
-        def add_bias(i):
-            y = y_pool.tile([P, COLS], F32, tag="y")
-            y_tiles[i] = y
+        def slope_branch(i):
+            slope = slope_pool.tile([P, O_STRIPES, BANK], F32, tag="slope")
+            slopes[i] = slope
             for a in range(O_STRIPES):
-                cols = slice(a * BANK, (a + 1) * BANK)
-                nc.vector.scalar_tensor_tensor(
-                    out=y[:, cols].rearrange("p (o f) -> p o f", f=FREQ),
-                    in0=z_banks[(i, a)][:].rearrange("p f o -> p o f"),
-                    scalar=sign[:, 0:1],
-                    in1=bias_s[:, cols].rearrange("p (o f) -> p o f", f=FREQ),
-                    op0=ALU.mult,
-                    op1=ALU.add,
+                nc.scalar.activation(
+                    out=slope[:, a, :],
+                    in_=z_banks[(i, a)][:],
+                    func=ACT.Identity,
+                    bias=slope_bias_col[:, a : a + 1],
+                    scale=alpha_t[:, 0:1],
                 )
 
-        def prelu(i):
-            y = y_tiles[i]
-            total = small.tile([P, 1], F32, tag="total")
-            nc.vector.scalar_tensor_tensor(
-                out=y[:], in0=y[:], scalar=alpha_t[:, 0:1], in1=y[:], op0=ALU.mult, op1=ALU.max, accum_out=total[:]
-            )
-            totals[i] = total
+        def prelu_and_turn(i):
+            p_tile = p_pool.tile([P, O_STRIPES, FREQ, P], F32, tag="p")
+            p_tiles[i] = p_tile
+            total = setup_pool.tile([P, BANK], F32, tag="setup", name="total")
+            sums[i] = total
+            for a in range(O_STRIPES):
+                nc.vector.scalar_tensor_tensor(
+                    out=p_tile[:, a, :, :].rearrange("p f t -> p (f t)"),
+                    in0=z_banks[(i, a)][:],
+                    scalar=bias_col[:, a : a + 1],
+                    in1=slopes[i][:, a, :],
+                    op0=ALU.add,
+                    op1=ALU.max,
+                )
+                pt = pt_pool.tile([P, FREQ, P], F32, tag="pt")
+                pt_banks[(i, a)] = pt
+                for f in range(FREQ):
+                    nc.tensor.transpose(pt[:, f, :], p_tile[:, a, f, :], ident[:])
+                for f in range(FREQ):
+                    nc.tensor.matmul(
+                        out=total[:, 0:P],
+                        lhsT=p_tile[:, a, f, :],
+                        rhs=ident[:],
+                        is_transpose=True,
+                        start=(a == 0 and f == 0),
+                        stop=(a == O_STRIPES - 1 and f == FREQ - 1),
+                    )
 
         def mean(i):
             neg_mean = small.tile([P, 1], F32, tag="neg_mean")
-            nc.vector.tensor_scalar(out=neg_mean[:], in0=totals[i][:], scalar1=-1.0 / COLS, scalar2=None, op0=ALU.mult)
+            folded = square_pool.tile([P, P], F32, tag="folded")
+            nc.scalar.activation(out=folded[:], in_=sums[i][:, 0:P], func=ACT.Copy, scale=-1.0 / COLS, accum_out=neg_mean[:])
             neg_means[i] = neg_mean
 
         def deviation(i):
-            square = square_pool.tile([P, COLS], BF16, tag="square")
+            parts = small.tile([P, O_STRIPES], F32, tag="parts")
+            squares[i] = parts
+            for a in range(O_STRIPES):
+                square = square_pool.tile([P, BANK], BF16, tag="square")
+                nc.scalar.activation(
+                    out=square[:],
+                    in_=pt_banks[(i, a)][:].rearrange("p f o -> p (f o)"),
+                    func=ACT.Square,
+                    bias=neg_means[i][:, 0:1],
+                    scale=1.0,
+                    accum_out=parts[:, a : a + 1],
+                )
+
+        def add_squares(i):
             total_sq = small.tile([P, 1], F32, tag="total_sq")
-            nc.scalar.activation(
-                out=square[:], in_=y_tiles[i][:], func=ACT.Square, bias=neg_means[i][:, 0:1], scale=1.0, accum_out=total_sq[:]
+            nc.gpsimd.tensor_scalar(
+                out=total_sq[:],
+                in0=squares[i][:, 0:1],
+                scalar1=squares[i][:, 1:2],
+                scalar2=squares[i][:, 2:3],
+                op0=ALU.add,
+                op1=ALU.add,
             )
+            totals_sq[i] = total_sq
+
+        def inverse_deviation(i):
             rstd = small.tile([P, 1], F32, tag="rstd")
             nc.scalar.activation(
-                out=rstd[:], in_=total_sq[:], func=ACT.Abs_reciprocal_sqrt, bias=eps_t[:, 0:1], scale=1.0 / COLS
+                out=rstd[:], in_=totals_sq[i][:], func=ACT.Abs_reciprocal_sqrt, bias=eps_t[:, 0:1], scale=1.0 / COLS
             )
             rstds[i] = rstd
 
         def centre_and_gain(i):
             n = n_pool.tile([P, COLS], F32, tag="n")
-            for k in range(BANKS):
-                cols = slice(k * BANK, (k + 1) * BANK)
+            for a in range(O_STRIPES):
+                cols = slice(a * BANK, (a + 1) * BANK)
                 nc.vector.scalar_tensor_tensor(
-                    out=n[:, cols],
-                    in0=y_tiles[i][:, cols],
+                    out=n[:, cols].rearrange("p (o f) -> p o f", f=FREQ),
+                    in0=pt_banks[(i, a)][:].rearrange("p f o -> p o f"),
                     scalar=neg_means[i][:, 0:1],
-                    in1=gamma_banks[k][:],
+                    in1=gamma_t[:, cols].rearrange("p (o f) -> p o f", f=FREQ),
                     op0=ALU.add,
                     op1=ALU.mult,
                 )
@@ -260,40 +316,51 @@ def tile_unified2dattentiononframe_pa_t_kernel(
                     in_=heads[:, first_head:end_head, s, :],
                 )
 
-        regroup(0, 0, nc.scalar.copy)
-        nc.scalar.activation(
-            out=bias_s[:].rearrange("p (o f) -> p o f", f=FREQ),
-            in_=bias_bank[:, ROW_BIAS : ROW_BIAS + OUT_CH].unsqueeze(2).to_broadcast([P, OUT_CH, FREQ]),
-            func=ACT.Copy,
-            scale=sign[:, 0:1],
-        )
-        regroup(0, 1, nc.vector.tensor_copy)
+        regroup(0, 0, 0, P, nc.scalar.copy)
+        regroup(0, 1, 0, P, nc.scalar.copy)
+        nc.vector.tensor_scalar(out=w_signed[:], in0=w_grouped[:], scalar1=sign[:, 0:1], scalar2=None, op0=ALU.mult)
+        for g in range(PASSES):
+            for a in range(O_STRIPES):
+                first = (g * OUT_CH + a * P) * PACK
+                nc.vector.quantize_mx(
+                    out=w_codes[:, g, a * P : (a + 1) * P].bitcast(FP8X4),
+                    scales=w_scales[:, g, a * P : (a + 1) * P],
+                    in_=w_signed[:, first : first + P * PACK],
+                )
         quantise(0, 0)
         quantise(0, 1)
-        multiply(0)
-        regroup(1, 0, nc.scalar.copy)
-        regroup(1, 1, nc.scalar.copy)
         for k in range(BANKS):
-            gamma_bank = gamma_pool.tile([P, BANK], F32, tag="gamma%d" % k, name="gamma_bank")
+            gamma_bank = pt_pool.tile([P, BANK], F32, tag="pt", name="gamma_bank")
             spread(gamma_bank, signed_ones, ROW_GAMMA + k * BANK)
-            gamma_banks.append(gamma_bank)
+            nc.scalar.copy(out=gamma_t[:, k * BANK : (k + 1) * BANK], in_=gamma_bank[:])
         for k in range(BANKS):
-            beta_bank = setup_pool.tile([P, BANK], F32, tag="setup")
+            beta_bank = pt_pool.tile([P, BANK], F32, tag="pt", name="beta_bank")
             spread(beta_bank, ones, ROW_BETA + k * BANK)
             nc.scalar.copy(out=beta_t[:, k * BANK : (k + 1) * BANK], in_=beta_bank[:])
+        multiply(0)
+        bias_col = const.tile([P, O_STRIPES], F32)
+        nc.vector.tensor_copy(out=bias_col[:], in_=bias_cols_bank[:, 0:O_STRIPES])
+        slope_bias_col = const.tile([P, O_STRIPES], F32)
+        nc.vector.tensor_scalar(out=slope_bias_col[:], in0=bias_col[:], scalar1=alpha_t[:, 0:1], scalar2=None, op0=ALU.mult)
+        regroup(1, 0, 0, P, nc.vector.tensor_copy)
+        regroup(1, 1, 0, P, nc.vector.tensor_copy)
 
         for i in range(UNITS):
+            slope_branch(i)
+            if i > 0:
+                add_squares(i - 1)
+                inverse_deviation(i - 1)
+            prelu_and_turn(i)
             if i + 2 < UNITS:
                 b_next, tt_next = divmod(i + 2, T_STRIPES)
                 if tt_next == 0 and b_next + 1 < B:
                     new_x_tiles(b_next + 1)
                     load_x(b_next + 1, slice(0, T))
-                regroup(i + 2, 0, nc.scalar.copy)
-                regroup(i + 2, 1, nc.scalar.copy)
-            add_bias(i)
+                regroup_on_scalar(i + 2)
             if i + 1 < UNITS:
                 quantise(i + 1, 0)
-            prelu(i)
+            if i + 2 < UNITS:
+                regroup_on_vector(i + 2)
             if i + 1 < UNITS:
                 quantise(i + 1, 1)
                 multiply(i + 1)
@@ -307,6 +374,8 @@ def tile_unified2dattentiononframe_pa_t_kernel(
                 scale_and_shift(i - 1, 0, H)
                 store(i - 1, 0, H)
             centre_and_gain(i)
+        add_squares(UNITS - 1)
+        inverse_deviation(UNITS - 1)
         for piece in range(LAST_PIECES):
             first_head = piece * H // LAST_PIECES
             end_head = (piece + 1) * H // LAST_PIECES

@@ -29,9 +29,7 @@ BANK = 512
 BANKS = COLS // BANK
 HEAD_COLS = COLS // H
 
-VECTOR_HEADS = 2
 LAST_PIECES = 4
-VECTOR_STEPS = 96
 
 FLOPS = 2 * OUT_CH * CIN * B * FREQ * T
 
@@ -50,7 +48,8 @@ def tile_unified2dattentiononframe_pa_t_kernel(
     with ExitStack() as ctx:
         const = ctx.enter_context(tc.tile_pool(name="const", bufs=1))
         raw_pool = ctx.enter_context(tc.tile_pool(name="raw", bufs=2 * PASSES))
-        grouped_pool = ctx.enter_context(tc.tile_pool(name="grouped", bufs=2 * PASSES))
+        grouped_pool = ctx.enter_context(tc.tile_pool(name="grouped", bufs=2))
+        grouped_late_pool = ctx.enter_context(tc.tile_pool(name="grouped_late", bufs=1))
         code_pool = ctx.enter_context(tc.tile_pool(name="codes", bufs=3))
         slope_pool = ctx.enter_context(tc.tile_pool(name="slope", bufs=2))
         p_pool = ctx.enter_context(tc.tile_pool(name="p", bufs=2))
@@ -157,22 +156,15 @@ def tile_unified2dattentiononframe_pa_t_kernel(
         gamma_t = const.tile([P, COLS], F32)
         beta_t = const.tile([P, COLS], F32)
 
-        def regroup(i, g, first_step, end_step, copy):
+        def copy_on_gpsimd(out, in_):
+            nc.gpsimd.tensor_scalar(out=out, in0=in_, scalar1=1.0, scalar2=0.0, op0=ALU.mult, op1=ALU.add)
+
+        def regroup(i, g, copy):
             b, tt = divmod(i, T_STRIPES)
-            if (i, g) not in grouped:
-                side = grouped_pool.tile([P, FREQ, P, PACK], BF16, tag="grouped", name="side", align_bytes=64)
-                grouped[(i, g)] = side
-            copy(
-                out=grouped[(i, g)][:, :, first_step:end_step, :],
-                in_=raw[(b, g)][:, :, :, tt * P + first_step : tt * P + end_step].rearrange("p j f t -> p f t j"),
-            )
-
-        def regroup_on_scalar(i):
-            regroup(i, 0, 0, P, nc.scalar.copy)
-            regroup(i, 1, VECTOR_STEPS, P, nc.scalar.copy)
-
-        def regroup_on_vector(i):
-            regroup(i, 1, 0, VECTOR_STEPS, nc.vector.tensor_copy)
+            pool = grouped_pool if g == 0 else grouped_late_pool
+            side = pool.tile([P, FREQ, P, PACK], BF16, tag="grouped", name="side", align_bytes=64)
+            grouped[(i, g)] = side
+            copy(out=side[:], in_=raw[(b, g)][:, :, :, tt * P : (tt + 1) * P].rearrange("p j f t -> p f t j"))
 
         def quantise(i, g):
             if g == 0:
@@ -301,12 +293,6 @@ def tile_unified2dattentiononframe_pa_t_kernel(
                 out=n[:, cols], in0=n[:, cols], scalar=rstds[i][:, 0:1], in1=beta_t[:, cols], op0=ALU.mult, op1=ALU.add
             )
 
-        def scale_then_shift_on_gpsimd(i, first_head, end_head):
-            cols = slice(first_head * HEAD_COLS, end_head * HEAD_COLS)
-            n = n_tiles[i]
-            nc.vector.tensor_scalar(out=n[:, cols], in0=n[:, cols], scalar1=rstds[i][:, 0:1], scalar2=None, op0=ALU.mult)
-            nc.gpsimd.tensor_tensor(out=n[:, cols], in0=n[:, cols], in1=beta_t[:, cols], op=ALU.add)
-
         def store(i, first_head, end_head):
             b, tt = divmod(i, T_STRIPES)
             heads = n_tiles[i][:].rearrange("p (h s d) -> p h s d", h=H, s=len(outs), d=HD)
@@ -316,8 +302,8 @@ def tile_unified2dattentiononframe_pa_t_kernel(
                     in_=heads[:, first_head:end_head, s, :],
                 )
 
-        regroup(0, 0, 0, P, nc.scalar.copy)
-        regroup(0, 1, 0, P, nc.scalar.copy)
+        regroup(0, 0, nc.scalar.copy)
+        regroup(0, 1, nc.scalar.copy)
         nc.vector.tensor_scalar(out=w_signed[:], in0=w_grouped[:], scalar1=sign[:, 0:1], scalar2=None, op0=ALU.mult)
         for g in range(PASSES):
             for a in range(O_STRIPES):
@@ -342,13 +328,12 @@ def tile_unified2dattentiononframe_pa_t_kernel(
         nc.vector.tensor_copy(out=bias_col[:], in_=bias_cols_bank[:, 0:O_STRIPES])
         slope_bias_col = const.tile([P, O_STRIPES], F32)
         nc.vector.tensor_scalar(out=slope_bias_col[:], in0=bias_col[:], scalar1=alpha_t[:, 0:1], scalar2=None, op0=ALU.mult)
-        regroup(1, 0, 0, P, nc.vector.tensor_copy)
-        regroup(1, 1, 0, P, nc.vector.tensor_copy)
+        regroup(1, 0, nc.vector.tensor_copy)
+        regroup(1, 1, nc.vector.tensor_copy)
 
         for i in range(UNITS):
             slope_branch(i)
             if i > 0:
-                add_squares(i - 1)
                 inverse_deviation(i - 1)
             prelu_and_turn(i)
             if i + 2 < UNITS:
@@ -356,25 +341,21 @@ def tile_unified2dattentiononframe_pa_t_kernel(
                 if tt_next == 0 and b_next + 1 < B:
                     new_x_tiles(b_next + 1)
                     load_x(b_next + 1, slice(0, T))
-                regroup_on_scalar(i + 2)
+                regroup(i + 2, 0, nc.scalar.copy)
             if i + 1 < UNITS:
                 quantise(i + 1, 0)
-            if i + 2 < UNITS:
-                regroup_on_vector(i + 2)
+            if i > 0:
+                scale_and_shift(i - 1, 0, H)
+                store(i - 1, 0, H)
             if i + 1 < UNITS:
                 quantise(i + 1, 1)
                 multiply(i + 1)
+            if i + 2 < UNITS:
+                regroup(i + 2, 1, copy_on_gpsimd)
             mean(i)
             deviation(i)
-            if 0 < i < UNITS - 1:
-                scale_and_shift(i - 1, 0, VECTOR_HEADS)
-                scale_then_shift_on_gpsimd(i - 1, VECTOR_HEADS, H)
-                store(i - 1, 0, H)
-            if i == UNITS - 1:
-                scale_and_shift(i - 1, 0, H)
-                store(i - 1, 0, H)
+            add_squares(i)
             centre_and_gain(i)
-        add_squares(UNITS - 1)
         inverse_deviation(UNITS - 1)
         for piece in range(LAST_PIECES):
             first_head = piece * H // LAST_PIECES

@@ -178,20 +178,20 @@ def tile_unified2dattentiononframe_pa_t_kernel(
                 in_=grouped[(i, g)][:].rearrange("p f t j -> p (f t j)"),
             )
 
-        def multiply(i):
+        def multiply(i, g):
             for a in range(O_STRIPES):
-                z = z_pool.tile([P, BANK], F32, tag="z")
-                for g in range(PASSES):
-                    nc.tensor.matmul_mx(
-                        out=z[:],
-                        lhsT=w_codes[:, g, a * P : (a + 1) * P].bitcast(FP8X4),
-                        lhsT_scale=w_scales[:, g, a * P : (a + 1) * P],
-                        rhs=x_codes[i][:, g, :].bitcast(FP8X4),
-                        rhs_scale=x_scales[i][:, g, :],
-                        start=(g == 0),
-                        stop=(g == PASSES - 1),
-                    )
-                z_banks[(i, a)] = z
+                if g == 0:
+                    z = z_pool.tile([P, BANK], F32, tag="z")
+                    z_banks[(i, a)] = z
+                nc.tensor.matmul_mx(
+                    out=z_banks[(i, a)][:],
+                    lhsT=w_codes[:, g, a * P : (a + 1) * P].bitcast(FP8X4),
+                    lhsT_scale=w_scales[:, g, a * P : (a + 1) * P],
+                    rhs=x_codes[i][:, g, :].bitcast(FP8X4),
+                    rhs_scale=x_scales[i][:, g, :],
+                    start=(g == 0),
+                    stop=(g == PASSES - 1),
+                )
 
         def slope_branch(i):
             slope = slope_pool.tile([P, O_STRIPES, BANK], F32, tag="slope")
@@ -323,7 +323,8 @@ def tile_unified2dattentiononframe_pa_t_kernel(
             beta_bank = pt_pool.tile([P, BANK], F32, tag="pt", name="beta_bank")
             spread(beta_bank, ones, ROW_BETA + k * BANK)
             nc.scalar.copy(out=beta_t[:, k * BANK : (k + 1) * BANK], in_=beta_bank[:])
-        multiply(0)
+        multiply(0, 0)
+        multiply(0, 1)
         bias_col = const.tile([P, O_STRIPES], F32)
         nc.vector.tensor_copy(out=bias_col[:], in_=bias_cols_bank[:, 0:O_STRIPES])
         slope_bias_col = const.tile([P, O_STRIPES], F32)
@@ -344,12 +345,13 @@ def tile_unified2dattentiononframe_pa_t_kernel(
                 regroup(i + 2, 0, nc.scalar.copy)
             if i + 1 < UNITS:
                 quantise(i + 1, 0)
+                multiply(i + 1, 0)
             if i > 0:
                 scale_and_shift(i - 1, 0, H)
                 store(i - 1, 0, H)
             if i + 1 < UNITS:
                 quantise(i + 1, 1)
-                multiply(i + 1)
+                multiply(i + 1, 1)
             if i + 2 < UNITS:
                 regroup(i + 2, 1, copy_on_gpsimd)
             mean(i)

@@ -253,19 +253,11 @@ def tile_unified2dattentiononframe_pa_t_kernel(
                     accum_out=parts[:, a : a + 1],
                 )
 
-        def add_squares(i):
-            total_sq = small.tile([P, 1], F32, tag="total_sq")
-            nc.gpsimd.tensor_scalar(
-                out=total_sq[:],
-                in0=squares[i][:, 0:1],
-                scalar1=squares[i][:, 1:2],
-                scalar2=squares[i][:, 2:3],
-                op0=ALU.add,
-                op1=ALU.add,
-            )
-            totals_sq[i] = total_sq
-
         def inverse_deviation(i):
+            total_sq = small.tile([P, 1], F32, tag="total_sq")
+            parts_copy = small.tile([P, O_STRIPES], F32, tag="parts_copy")
+            nc.scalar.activation(out=parts_copy[:], in_=squares[i][:], func=ACT.Copy, accum_out=total_sq[:])
+            totals_sq[i] = total_sq
             rstd = small.tile([P, 1], F32, tag="rstd")
             nc.scalar.activation(
                 out=rstd[:], in_=totals_sq[i][:], func=ACT.Abs_reciprocal_sqrt, bias=eps_t[:, 0:1], scale=1.0 / COLS
@@ -346,17 +338,15 @@ def tile_unified2dattentiononframe_pa_t_kernel(
             if i + 1 < UNITS:
                 quantise(i + 1, 0)
                 multiply(i + 1, 0)
-            if i > 0:
-                scale_and_shift(i - 1, 0, H)
-                store(i - 1, 0, H)
-            if i + 1 < UNITS:
                 quantise(i + 1, 1)
                 multiply(i + 1, 1)
             if i + 2 < UNITS:
                 regroup(i + 2, 1, copy_on_gpsimd)
+            if i > 0:
+                scale_and_shift(i - 1, 0, H)
+                store(i - 1, 0, H)
             mean(i)
             deviation(i)
-            add_squares(i)
             centre_and_gain(i)
         inverse_deviation(UNITS - 1)
         for piece in range(LAST_PIECES):

@@ -31,6 +31,8 @@ HEAD_COLS = COLS // H
 
 LAST_PIECES = 4
 
+RUN = 4
+
 FLOPS = 2 * OUT_CH * CIN * B * FREQ * T
 
 ROW_BIAS = 0
@@ -164,7 +166,11 @@ def tile_unified2dattentiononframe_pa_t_kernel(
             pool = grouped_pool if g == 0 else grouped_late_pool
             side = pool.tile([P, FREQ, P, PACK], BF16, tag="grouped", name="side", align_bytes=64)
             grouped[(i, g)] = side
-            copy(out=side[:], in_=raw[(b, g)][:, :, :, tt * P : (tt + 1) * P].rearrange("p j f t -> p f t j"))
+            run = 1 if copy == copy_on_gpsimd else RUN
+            copy(
+                out=side[:].rearrange("p f (c i) j -> p f c j i", i=run),
+                in_=raw[(b, g)][:, :, :, tt * P : (tt + 1) * P].rearrange("p j f (c i) -> p f c j i", i=run),
+            )
 
         def quantise(i, g):
             if g == 0:

@@ -31,6 +31,7 @@ HEAD_COLS = COLS // H
 
 LAST_PIECES = 4
 
+EARLY_STEPS = 96
 RUN = 4
 
 FLOPS = 2 * OUT_CH * CIN * B * FREQ * T
@@ -161,15 +162,18 @@ def tile_unified2dattentiononframe_pa_t_kernel(
         def copy_on_gpsimd(out, in_):
             nc.gpsimd.tensor_scalar(out=out, in0=in_, scalar1=1.0, scalar2=0.0, op0=ALU.mult, op1=ALU.add)
 
-        def regroup(i, g, copy):
+        def regroup(i, g, copy, first_step=0, end_step=P):
             b, tt = divmod(i, T_STRIPES)
-            pool = grouped_pool if g == 0 else grouped_late_pool
-            side = pool.tile([P, FREQ, P, PACK], BF16, tag="grouped", name="side", align_bytes=64)
-            grouped[(i, g)] = side
+            if (i, g) not in grouped:
+                pool = grouped_pool if g == 0 else grouped_late_pool
+                side = pool.tile([P, FREQ, P, PACK], BF16, tag="grouped", name="side", align_bytes=64)
+                grouped[(i, g)] = side
             run = 1 if copy == copy_on_gpsimd else RUN
             copy(
-                out=side[:].rearrange("p f (c i) j -> p f c j i", i=run),
-                in_=raw[(b, g)][:, :, :, tt * P : (tt + 1) * P].rearrange("p j f (c i) -> p f c j i", i=run),
+                out=grouped[(i, g)][:, :, first_step:end_step, :].rearrange("p f (c i) j -> p f c j i", i=run),
+                in_=raw[(b, g)][:, :, :, tt * P + first_step : tt * P + end_step].rearrange(
+                    "p j f (c i) -> p f c j i", i=run
+                ),
             )
 
         def quantise(i, g):
@@ -199,17 +203,17 @@ def tile_unified2dattentiononframe_pa_t_kernel(
                     stop=(g == PASSES - 1),
                 )
 
-        def slope_branch(i):
-            slope = slope_pool.tile([P, O_STRIPES, BANK], F32, tag="slope")
-            slopes[i] = slope
-            for a in range(O_STRIPES):
-                nc.scalar.activation(
-                    out=slope[:, a, :],
-                    in_=z_banks[(i, a)][:],
-                    func=ACT.Identity,
-                    bias=slope_bias_col[:, a : a + 1],
-                    scale=alpha_t[:, 0:1],
-                )
+        def slope_branch(i, a):
+            if a == 0:
+                slope = slope_pool.tile([P, O_STRIPES, BANK], F32, tag="slope")
+                slopes[i] = slope
+            nc.scalar.activation(
+                out=slopes[i][:, a, :],
+                in_=z_banks[(i, a)][:],
+                func=ACT.Identity,
+                bias=slope_bias_col[:, a : a + 1],
+                scale=alpha_t[:, 0:1],
+            )
 
         def prelu_and_turn(i):
             p_tile = p_pool.tile([P, O_STRIPES, FREQ, P], F32, tag="p")
@@ -259,11 +263,13 @@ def tile_unified2dattentiononframe_pa_t_kernel(
                     accum_out=parts[:, a : a + 1],
                 )
 
-        def inverse_deviation(i):
+        def add_squares(i):
             total_sq = small.tile([P, 1], F32, tag="total_sq")
             parts_copy = small.tile([P, O_STRIPES], F32, tag="parts_copy")
             nc.scalar.activation(out=parts_copy[:], in_=squares[i][:], func=ACT.Copy, accum_out=total_sq[:])
             totals_sq[i] = total_sq
+
+        def inverse_deviation(i):
             rstd = small.tile([P, 1], F32, tag="rstd")
             nc.scalar.activation(
                 out=rstd[:], in_=totals_sq[i][:], func=ACT.Abs_reciprocal_sqrt, bias=eps_t[:, 0:1], scale=1.0 / COLS
@@ -331,16 +337,20 @@ def tile_unified2dattentiononframe_pa_t_kernel(
         regroup(1, 1, nc.vector.tensor_copy)
 
         for i in range(UNITS):
-            slope_branch(i)
+            slope_branch(i, 0)
+            if i > 0:
+                add_squares(i - 1)
+            slope_branch(i, 1)
             if i > 0:
                 inverse_deviation(i - 1)
+            slope_branch(i, 2)
             prelu_and_turn(i)
             if i + 2 < UNITS:
                 b_next, tt_next = divmod(i + 2, T_STRIPES)
                 if tt_next == 0 and b_next + 1 < B:
                     new_x_tiles(b_next + 1)
                     load_x(b_next + 1, slice(0, T))
-                regroup(i + 2, 0, nc.scalar.copy)
+                regroup(i + 2, 0, nc.scalar.copy, 0, EARLY_STEPS)
             if i + 1 < UNITS:
                 quantise(i + 1, 0)
                 multiply(i + 1, 0)
@@ -352,8 +362,11 @@ def tile_unified2dattentiononframe_pa_t_kernel(
                 scale_and_shift(i - 1, 0, H)
                 store(i - 1, 0, H)
             mean(i)
+            if i + 2 < UNITS:
+                regroup(i + 2, 0, nc.scalar.copy, EARLY_STEPS, P)
             deviation(i)
             centre_and_gain(i)
+        add_squares(UNITS - 1)
         inverse_deviation(UNITS - 1)
         for piece in range(LAST_PIECES):
             first_head = piece * H // LAST_PIECES

from contextlib import ExitStack

import concourse.mybir as mybir
from concourse.masks import make_identity

F32 = mybir.dt.float32
BF16 = mybir.dt.bfloat16
U32 = mybir.dt.uint32
U8 = mybir.dt.uint8
FP8X4 = mybir.dt.float8_e4m3fn_x4
ALU = mybir.AluOpType
ACT = mybir.ActivationFunctionType

B, CIN, HID, FREQ, T, H = 4, 1024, 128, 4, 512, 8
OUT_CH = 3 * HID
HD = HID * FREQ // H
EPS = 1e-5

P = 128
PACK = 4
K_PASS = P * PACK
PASSES = CIN // K_PASS
PAIRS = PACK // 2
O_STRIPES = OUT_CH // P
T_STRIPES = T // P
UNITS = B * T_STRIPES
COLS = OUT_CH * FREQ
BANK = 512
BANKS = COLS // BANK
HEAD_COLS = COLS // H

LAST_PIECES = 4

EARLY_STEPS = 96
RUN = 4

FLOPS = 2 * OUT_CH * CIN * B * FREQ * T

ROW_BIAS = 0
ROW_ALPHA = OUT_CH
ROW_GAMMA = BANK
ROW_BETA = BANK + COLS
ROW_COLS = BANK + 2 * COLS


def tile_unified2dattentiononframe_pa_t_kernel(
    tc, x, qkv_w, qkv_b, qkv_alpha, qkv_gamma, qkv_beta, out_0, out_1, out_2
):
    nc = tc.nc
    outs = (out_0, out_1, out_2)
    with ExitStack() as ctx:
        const = ctx.enter_context(tc.tile_pool(name="const", bufs=1))
        raw_pool = ctx.enter_context(tc.tile_pool(name="raw", bufs=2 * PASSES))
        grouped_pool = ctx.enter_context(tc.tile_pool(name="grouped", bufs=2))
        grouped_late_pool = ctx.enter_context(tc.tile_pool(name="grouped_late", bufs=1))
        code_pool = ctx.enter_context(tc.tile_pool(name="codes", bufs=3))
        slope_pool = ctx.enter_context(tc.tile_pool(name="slope", bufs=2))
        p_pool = ctx.enter_context(tc.tile_pool(name="p", bufs=2))
        n_pool = ctx.enter_context(tc.tile_pool(name="n", bufs=4))
        small = ctx.enter_context(tc.tile_pool(name="small", bufs=4))
        square_pool = ctx.enter_context(tc.tile_pool(name="square", bufs=2))
        z_pool = ctx.enter_context(tc.psum_pool(name="z", bufs=BANKS))
        pt_pool = ctx.enter_context(tc.psum_pool(name="pt", bufs=BANKS))
        setup_pool = ctx.enter_context(tc.psum_pool(name="setup", bufs=2))
        ctx.enter_context(tc.manual_schedule())

        raw = {}

        def new_x_tiles(b):
            for g in range(PASSES):
                chunk = raw_pool.tile([P, PACK, FREQ, T], BF16, tag="raw", name="chunk")
                raw[(b, g)] = chunk

        def load_x(b, t_range):
            for g in range(PASSES):
                nc.sync.dma_start(
                    out=raw[(b, g)][:, :, :, t_range],
                    in_=x[b, g * K_PASS : (g + 1) * K_PASS, :, t_range].rearrange("(p j) f t -> p j f t", j=PACK),
                )

        rows = const.tile([P, ROW_COLS], BF16)
        nc.vector.memset(rows[:], 0.0)
        ones = const.tile([P, P], BF16)
        nc.vector.memset(ones[:], 1.0)
        eps_t = const.tile([P, 1], F32)
        nc.vector.memset(eps_t[:], EPS)
        w_sb = const.tile([P, O_STRIPES * CIN], BF16)
        nc.sync.dma_start(
            out=w_sb[:].rearrange("p (a c) -> p a c", a=O_STRIPES),
            in_=qkv_w.rearrange("(a p) c -> p a c", p=P),
        )
        new_x_tiles(0)
        load_x(0, slice(0, P))
        nc.sync.dma_start(out=rows[0:1, ROW_ALPHA : ROW_ALPHA + 1], in_=qkv_alpha.rearrange("(r o) -> r o", r=1))
        nc.sync.dma_start(out=rows[0:1, ROW_BIAS : ROW_BIAS + OUT_CH], in_=qkv_b.rearrange("(r o) -> r o", r=1))
        nc.sync.dma_start(out=rows[0:1, ROW_GAMMA : ROW_GAMMA + COLS], in_=qkv_gamma.rearrange("r o c f -> r (o c f)"))
        nc.sync.dma_start(out=rows[0:1, ROW_BETA : ROW_BETA + COLS], in_=qkv_beta.rearrange("r o c f -> r (o c f)"))
        for tt in range(1, T_STRIPES):
            load_x(0, slice(tt * P, (tt + 1) * P))
        new_x_tiles(1)
        load_x(1, slice(0, T))

        warm = const.tile([P, 1], F32)
        nc.scalar.activation(out=warm[:], in_=eps_t[:], func=ACT.Abs_reciprocal_sqrt)

        ident = const.tile([P, P], F32)
        make_identity(nc, ident[:])

        w_pairs = w_sb[:].bitcast(F32).rearrange("p (a g q u) -> p a g q u", a=O_STRIPES, g=PASSES, q=P, u=PAIRS)
        w_grouped = const.tile([P, PASSES * OUT_CH * PACK], BF16, align_bytes=64)
        w_grouped_pairs = w_grouped[:].bitcast(F32).rearrange("p (g o u) -> p g o u", g=PASSES, o=OUT_CH, u=PAIRS)
        w_signed = const.tile([P, PASSES * OUT_CH * PACK], BF16, align_bytes=64)
        w_codes = const.tile([P, PASSES, OUT_CH], U32, align_bytes=64)
        w_scales = const.tile([P, PASSES, OUT_CH], U8, align_bytes=64)
        for g in range(PASSES):
            for a in range(O_STRIPES):
                wt = z_pool.tile([P, PAIRS, P], F32, tag="z", name="wt")
                for u in range(PAIRS):
                    nc.tensor.transpose(wt[:, u, :], w_pairs[:, a, g, :, u], ident[:])
                nc.vector.tensor_copy(
                    out=w_grouped_pairs[:, g, a * P : (a + 1) * P, :], in_=wt[:].rearrange("p u o -> p o u")
                )

        def spread(bank, factor, first_col):
            nc.tensor.matmul(out=bank[:], lhsT=factor[:], rhs=rows[:, first_col : first_col + BANK], start=True, stop=True)

        alpha_t = const.tile([P, 1], F32)
        sign = const.tile([P, 1], F32)
        bias_bank = setup_pool.tile([P, BANK], F32, tag="setup")
        spread(bias_bank, ones, ROW_BIAS)
        nc.vector.tensor_copy(out=alpha_t[:], in_=bias_bank[:, ROW_ALPHA : ROW_ALPHA + 1])
        nc.vector.tensor_scalar(out=sign[:], in0=alpha_t[:], scalar1=1.0, scalar2=2.0, op0=ALU.is_le, op1=ALU.mult)
        nc.vector.tensor_scalar(out=sign[:], in0=sign[:], scalar1=-1.0, scalar2=None, op0=ALU.add)
        signed_ones = const.tile([P, P], BF16)
        nc.vector.tensor_scalar(out=signed_ones[:], in0=ones[:], scalar1=sign[:, 0:1], scalar2=None, op0=ALU.mult)
        bias_cols_bank = setup_pool.tile([P, BANK], F32, tag="setup")
        for a in range(O_STRIPES):
            nc.tensor.matmul(
                out=bias_cols_bank[:, a : a + 1],
                lhsT=rows[:, ROW_BIAS + a * P : ROW_BIAS + (a + 1) * P],
                rhs=signed_ones[:, 0:1],
                start=True,
                stop=True,
            )

        grouped = {}
        x_codes = {}
        x_scales = {}
        z_banks = {}
        slopes = {}
        p_tiles = {}
        pt_banks = {}
        sums = {}
        n_tiles = {}
        neg_means = {}
        squares = {}
        totals_sq = {}
        rstds = {}
        gamma_t = const.tile([P, COLS], F32)
        beta_t = const.tile([P, COLS], F32)

        def copy_on_gpsimd(out, in_):
            nc.gpsimd.tensor_scalar(out=out, in0=in_, scalar1=1.0, scalar2=0.0, op0=ALU.mult, op1=ALU.add)

        def regroup(i, g, copy, first_step=0, end_step=P):
            b, tt = divmod(i, T_STRIPES)
            if (i, g) not in grouped:
                pool = grouped_pool if g == 0 else grouped_late_pool
                side = pool.tile([P, FREQ, P, PACK], BF16, tag="grouped", name="side", align_bytes=64)
                grouped[(i, g)] = side
            run = 1 if copy == copy_on_gpsimd else RUN
            copy(
                out=grouped[(i, g)][:, :, first_step:end_step, :].rearrange("p f (c i) j -> p f c j i", i=run),
                in_=raw[(b, g)][:, :, :, tt * P + first_step : tt * P + end_step].rearrange(
                    "p j f (c i) -> p f c j i", i=run
                ),
            )

        def quantise(i, g):
            if g == 0:
                codes = code_pool.tile([P, PASSES, FREQ * P], U32, tag="codes", align_bytes=64)
                scales = code_pool.tile([P, PASSES, FREQ * P], U8, tag="scales", align_bytes=64)
                x_codes[i] = codes
                x_scales[i] = scales
            nc.vector.quantize_mx(
                out=x_codes[i][:, g, :].bitcast(FP8X4),
                scales=x_scales[i][:, g, :],
                in_=grouped[(i, g)][:].rearrange("p f t j -> p (f t j)"),
            )

        def multiply(i, g):
            for a in range(O_STRIPES):
                if g == 0:
                    z = z_pool.tile([P, BANK], F32, tag="z")
                    z_banks[(i, a)] = z
                nc.tensor.matmul_mx(
                    out=z_banks[(i, a)][:],
                    lhsT=w_codes[:, g, a * P : (a + 1) * P].bitcast(FP8X4),
                    lhsT_scale=w_scales[:, g, a * P : (a + 1) * P],
                    rhs=x_codes[i][:, g, :].bitcast(FP8X4),
                    rhs_scale=x_scales[i][:, g, :],
                    start=(g == 0),
                    stop=(g == PASSES - 1),
                )

        def slope_branch(i, a):
            if a == 0:
                slope = slope_pool.tile([P, O_STRIPES, BANK], F32, tag="slope")
                slopes[i] = slope
            nc.scalar.activation(
                out=slopes[i][:, a, :],
                in_=z_banks[(i, a)][:],
                func=ACT.Identity,
                bias=slope_bias_col[:, a : a + 1],
                scale=alpha_t[:, 0:1],
            )

        def prelu_and_turn(i):
            p_tile = p_pool.tile([P, O_STRIPES, FREQ, P], F32, tag="p")
            p_tiles[i] = p_tile
            total = setup_pool.tile([P, BANK], F32, tag="setup", name="total")
            sums[i] = total
            for a in range(O_STRIPES):
                nc.vector.scalar_tensor_tensor(
                    out=p_tile[:, a, :, :].rearrange("p f t -> p (f t)"),
                    in0=z_banks[(i, a)][:],
                    scalar=bias_col[:, a : a + 1],
                    in1=slopes[i][:, a, :],
                    op0=ALU.add,
                    op1=ALU.max,
                )
                pt = pt_pool.tile([P, FREQ, P], F32, tag="pt")
                pt_banks[(i, a)] = pt
                for f in range(FREQ):
                    nc.tensor.transpose(pt[:, f, :], p_tile[:, a, f, :], ident[:])
                for f in range(FREQ):
                    nc.tensor.matmul(
                        out=total[:, 0:P],
                        lhsT=p_tile[:, a, f, :],
                        rhs=ident[:],
                        is_transpose=True,
                        start=(a == 0 and f == 0),
                        stop=(a == O_STRIPES - 1 and f == FREQ - 1),
                    )

        def mean(i):
            neg_mean = small.tile([P, 1], F32, tag="neg_mean")
            folded = square_pool.tile([P, P], F32, tag="folded")
            nc.scalar.activation(out=folded[:], in_=sums[i][:, 0:P], func=ACT.Copy, scale=-1.0 / COLS, accum_out=neg_mean[:])
            neg_means[i] = neg_mean

        def deviation(i):
            parts = small.tile([P, O_STRIPES], F32, tag="parts")
            squares[i] = parts
            for a in range(O_STRIPES):
                square = square_pool.tile([P, BANK], BF16, tag="square")
                nc.scalar.activation(
                    out=square[:],
                    in_=pt_banks[(i, a)][:].rearrange("p f o -> p (f o)"),
                    func=ACT.Square,
                    bias=neg_means[i][:, 0:1],
                    scale=1.0,
                    accum_out=parts[:, a : a + 1],
                )

        def add_squares(i):
            total_sq = small.tile([P, 1], F32, tag="total_sq")
            parts_copy = small.tile([P, O_STRIPES], F32, tag="parts_copy")
            nc.scalar.activation(out=parts_copy[:], in_=squares[i][:], func=ACT.Copy, accum_out=total_sq[:])
            totals_sq[i] = total_sq

        def inverse_deviation(i):
            rstd = small.tile([P, 1], F32, tag="rstd")
            nc.scalar.activation(
                out=rstd[:], in_=totals_sq[i][:], func=ACT.Abs_reciprocal_sqrt, bias=eps_t[:, 0:1], scale=1.0 / COLS
            )
            rstds[i] = rstd

        def centre_and_gain(i):
            n = n_pool.tile([P, COLS], F32, tag="n")
            for a in range(O_STRIPES):
                cols = slice(a * BANK, (a + 1) * BANK)
                nc.vector.scalar_tensor_tensor(
                    out=n[:, cols].rearrange("p (o f) -> p o f", f=FREQ),
                    in0=pt_banks[(i, a)][:].rearrange("p f o -> p o f"),
                    scalar=neg_means[i][:, 0:1],
                    in1=gamma_t[:, cols].rearrange("p (o f) -> p o f", f=FREQ),
                    op0=ALU.add,
                    op1=ALU.mult,
                )
            n_tiles[i] = n

        def scale_and_shift(i, first_head, end_head):
            cols = slice(first_head * HEAD_COLS, end_head * HEAD_COLS)
            n = n_tiles[i]
            nc.vector.scalar_tensor_tensor(
                out=n[:, cols], in0=n[:, cols], scalar=rstds[i][:, 0:1], in1=beta_t[:, cols], op0=ALU.mult, op1=ALU.add
            )

        def store(i, first_head, end_head):
            b, tt = divmod(i, T_STRIPES)
            heads = n_tiles[i][:].rearrange("p (h s d) -> p h s d", h=H, s=len(outs), d=HD)
            for s, out in enumerate(outs):
                nc.sync.dma_start(
                    out=out[b, first_head:end_head, tt * P : (tt + 1) * P, :].rearrange("h t d -> t h d"),
                    in_=heads[:, first_head:end_head, s, :],
                )

        regroup(0, 0, nc.scalar.copy)
        regroup(0, 1, nc.scalar.copy)
        nc.vector.tensor_scalar(out=w_signed[:], in0=w_grouped[:], scalar1=sign[:, 0:1], scalar2=None, op0=ALU.mult)
        for g in range(PASSES):
            for a in range(O_STRIPES):
                first = (g * OUT_CH + a * P) * PACK
                nc.vector.quantize_mx(
                    out=w_codes[:, g, a * P : (a + 1) * P].bitcast(FP8X4),
                    scales=w_scales[:, g, a * P : (a + 1) * P],
                    in_=w_signed[:, first : first + P * PACK],
                )
        quantise(0, 0)
        quantise(0, 1)
        for k in range(BANKS):
            gamma_bank = pt_pool.tile([P, BANK], F32, tag="pt", name="gamma_bank")
            spread(gamma_bank, signed_ones, ROW_GAMMA + k * BANK)
            nc.scalar.copy(out=gamma_t[:, k * BANK : (k + 1) * BANK], in_=gamma_bank[:])
        for k in range(BANKS):
            beta_bank = pt_pool.tile([P, BANK], F32, tag="pt", name="beta_bank")
            spread(beta_bank, ones, ROW_BETA + k * BANK)
            nc.scalar.copy(out=beta_t[:, k * BANK : (k + 1) * BANK], in_=beta_bank[:])
        multiply(0, 0)
        multiply(0, 1)
        bias_col = const.tile([P, O_STRIPES], F32)
        nc.vector.tensor_copy(out=bias_col[:], in_=bias_cols_bank[:, 0:O_STRIPES])
        slope_bias_col = const.tile([P, O_STRIPES], F32)
        nc.vector.tensor_scalar(out=slope_bias_col[:], in0=bias_col[:], scalar1=alpha_t[:, 0:1], scalar2=None, op0=ALU.mult)
        regroup(1, 0, nc.vector.tensor_copy)
        regroup(1, 1, nc.vector.tensor_copy)

        for i in range(UNITS):
            slope_branch(i, 0)
            if i > 0:
                add_squares(i - 1)
            slope_branch(i, 1)
            if i > 0:
                inverse_deviation(i - 1)
            slope_branch(i, 2)
            prelu_and_turn(i)
            if i + 2 < UNITS:
                b_next, tt_next = divmod(i + 2, T_STRIPES)
                if tt_next == 0 and b_next + 1 < B:
                    new_x_tiles(b_next + 1)
                    load_x(b_next + 1, slice(0, T))
                regroup(i + 2, 0, nc.scalar.copy, 0, EARLY_STEPS)
            if i + 1 < UNITS:
                quantise(i + 1, 0)
                multiply(i + 1, 0)
                quantise(i + 1, 1)
                multiply(i + 1, 1)
            if i + 2 < UNITS:
                regroup(i + 2, 1, copy_on_gpsimd)
            if i > 0:
                scale_and_shift(i - 1, 0, H)
                store(i - 1, 0, H)
            mean(i)
            if i + 2 < UNITS:
                regroup(i + 2, 0, nc.scalar.copy, EARLY_STEPS, P)
            deviation(i)
            centre_and_gain(i)
        add_squares(UNITS - 1)
        inverse_deviation(UNITS - 1)
        for piece in range(LAST_PIECES):
            first_head = piece * H // LAST_PIECES
            end_head = (piece + 1) * H // LAST_PIECES
            scale_and_shift(UNITS - 1, first_head, end_head)
            store(UNITS - 1, first_head, end_head)
